import numpy as np
import ml_dtypes


def mxq(x, axis, fmt="e4m3"):
    dtype, down = {"e4m3": (ml_dtypes.float8_e4m3fn, 7), "e5m2": (ml_dtypes.float8_e5m2, 14)}[fmt]
    v = np.moveaxis(np.asarray(x, np.float32).astype(ml_dtypes.bfloat16).astype(np.float64), axis, -1)
    blocks = v.reshape(v.shape[:-1] + (-1, 32))
    amax = np.abs(blocks).max(-1, keepdims=True)
    byte = np.maximum(np.where(amax > 0, np.frexp(amax)[1] - 1 + 127, 0) - down, 1)
    scale = np.exp2(byte - 127.0)
    codes = (blocks / scale).astype(np.float32).astype(dtype).astype(np.float64)
    return np.moveaxis((codes * scale).reshape(v.shape), -1, axis)


BF16 = ml_dtypes.bfloat16


def bf(x):
    return np.asarray(x, np.float32).astype(BF16)


def f64(x):
    return np.asarray(x).astype(np.float64)


B, HP, WS, NH, DH, ND = 1, 32, 32, 4, 128, 4
N = WS * WS
C = NH * DH
BW = B * (HP // WS) ** 2
NEG = -1e9


def dir_allowed():
    idx = np.arange(N)
    r, c = idx // WS, idx % WS
    return np.stack([c[None, :] < c[:, None], c[None, :] > c[:, None], r[None, :] < r[:, None], r[None, :] > r[:, None]])


def setup_inputs():
    v = np.random.standard_normal((BW, N, NH, DH)) + 0.3 * np.random.standard_normal((NH, DH))
    return {"q": bf(np.random.standard_normal((BW, N, NH, DH)) * 1.4 / np.sqrt(DH)),
            "k_dir": bf(np.random.standard_normal((ND, BW, N, NH, DH)) * 1.4),
            "v": bf(v)}


def reference(q, k_dir, v):
    qh = f64(q).transpose(0, 2, 1, 3)
    vh = f64(v).transpose(0, 2, 1, 3)
    vq = mxq(vh, 2, "e4m3")
    allowed = dir_allowed()
    o = vh
    for j in range(ND):
        s = qh @ f64(k_dir)[j].transpose(0, 2, 3, 1)
        s = np.where(allowed[j], s, NEG)
        e = np.exp(s - s.max(-1, keepdims=True))
        o = o + (mxq(e, 3, "e4m3") @ vq) / e.sum(-1, keepdims=True)
    return (o / (ND + 1)).transpose(0, 2, 1, 3).reshape(BW, N, C)

@@ -1,0 +1,455 @@
+from contextlib import ExitStack
+
+import concourse.mybir as mybir
+from concourse.masks import make_identity
+
+F32 = mybir.dt.float32
+BF16 = mybir.dt.bfloat16
+U32 = mybir.dt.uint32
+U8 = mybir.dt.uint8
+FP8X4 = mybir.dt.float8_e4m3fn_x4
+ALU = mybir.AluOpType
+ACT = mybir.ActivationFunctionType
+AXIS_X = mybir.AxisListType.X
+
+P = 128
+SIDE = 32
+POSITIONS = SIDE * SIDE
+HEADS = 4
+WIDTH = 128
+CHANNELS = HEADS * WIDTH
+TILES = POSITIONS // P
+LINES = P // SIDE
+PACK = 4
+K_PASS = P * PACK
+PASSES = POSITIONS // K_PASS
+CHUNKS = K_PASS // P
+PAIR = 2
+HALVES = PACK // PAIR
+NEG = -1.0e9
+
+LEFT, RIGHT, UP, DOWN = 0, 1, 2, 3
+FLOPS = 2 * 2 * 4 * HEADS * POSITIONS * POSITIONS * WIDTH
+
+TILE_ORDER = [t for a in range(TILES // 2) for t in (a, TILES - 1 - a)]
+ROUND = CHUNKS
+
+TURN_LAG = 2
+QUANT_LAG = 3
+AT_NORMALISE = 0
+AT_FIRST_ROUND = 1
+AT_REGROUP_VALUES = 2
+AT_SECOND_ROUND = 3
+AT_TO_CHANNELS = 4
+AT_PREPARE = 5
+AT_TO_ROWS = 6
+AT_QUANTISE_VALUES = 6
+
+
+def sees_smaller(direction):
+    return direction in (LEFT, UP)
+
+
+def in_columns(direction):
+    return direction in (LEFT, RIGHT)
+
+
+def seen_keys(direction, i):
+    if sees_smaller(direction):
+        return 0, (i + 1) * P - SIDE
+    return i * P + SIDE, POSITIONS
+
+
+def pass_list(direction, i):
+    lo, hi = seen_keys(direction, i)
+    return list(range(lo // K_PASS, (hi - 1) // K_PASS + 1))
+
+
+def blind_tile(direction):
+    return 0 if sees_smaller(direction) else TILES - 1
+
+
+def blind_rows(direction):
+    return slice(0, SIDE) if sees_smaller(direction) else slice(P - SIDE, P)
+
+
+def tile_localdirectionalattention_pa_kernel(tc, q, k_dir, v, out):
+    nc = tc.nc
+    groups = [(d, h) for h in range(HEADS) for d in (LEFT, RIGHT)]
+    groups += [(d, h) for h in range(HEADS) for d in (UP, DOWN)]
+
+    with ExitStack() as ctx:
+        keep = ctx.enter_context(tc.tile_pool(name="keep", bufs=1))
+        operands = ctx.enter_context(tc.tile_pool(name="operands", bufs=2))
+        work = ctx.enter_context(tc.tile_pool(name="work", bufs=4))
+        psum_scores = ctx.enter_context(tc.psum_pool(name="psum_scores", bufs=5))
+        psum_turn = ctx.enter_context(tc.psum_pool(name="psum_turn", bufs=2))
+        psum_pv = ctx.enter_context(tc.psum_pool(name="psum_pv", bufs=1))
+
+        def load_in_columns(dst, src, h):
+            head = slice(h * WIDTH, (h + 1) * WIDTH)
+            by_line = src.rearrange("(r i l) h d -> l r i (h d)", r=SIDE, i=TILES, l=LINES)
+            for line in range(LINES):
+                nc.sync.dma_start(
+                    out=dst[line * SIDE : (line + 1) * SIDE, :, head], in_=by_line[line][:, :, head]
+                )
+
+        def load_in_rows(dst, src):
+            nc.sync.dma_start(out=dst[:], in_=src.rearrange("(i p) h d -> p i (h d)", p=P))
+
+        q_raw = {}
+        k_raw = {}
+        for columns in (True, False):
+            q_raw[columns] = keep.tile([P, TILES, CHANNELS], BF16, name="q_raw%d" % columns)
+        for direction in (LEFT, RIGHT, UP, DOWN):
+            k_raw[direction] = keep.tile([P, TILES, CHANNELS], BF16, name="k_raw%d" % direction)
+        v_keys_rows = keep.tile([P, PASSES * HALVES, PAIR, CHANNELS], BF16)
+        v_keys_columns = keep.tile([P, PAIR, PASSES * HALVES, CHANNELS], BF16)
+        v_rows = keep.tile([P, TILES, CHANNELS], BF16)
+
+        by_column = v[0].rearrange(
+            "(r b u c) h d -> c r (b u) (h d)", r=SIDE // PAIR, b=PAIR, u=PASSES * HALVES, c=8
+        )
+        for h in range(HEADS):
+            load_in_columns(q_raw[True], q[0], h)
+            load_in_columns(k_raw[LEFT], k_dir[LEFT, 0], h)
+            load_in_columns(k_raw[RIGHT], k_dir[RIGHT, 0], h)
+            if h == 0:
+                for c in range(8):
+                    nc.sync.dma_start(
+                        out=v_keys_columns[c * 16 : (c + 1) * 16].rearrange("p b u x -> p (b u) x"),
+                        in_=by_column[c],
+                    )
+        load_in_rows(q_raw[False], q[0])
+        load_in_rows(k_raw[UP], k_dir[UP, 0])
+        load_in_rows(v_rows, v[0])
+        nc.sync.dma_start(
+            out=v_keys_rows[:].rearrange("p u b x -> p u (b x)"),
+            in_=v[0].rearrange("(u p b) h d -> p u (b h d)", p=P, b=PAIR),
+        )
+        load_in_rows(k_raw[DOWN], k_dir[DOWN, 0])
+
+        ident_bf16 = keep.tile([P, P], BF16)
+        make_identity(nc, ident_bf16[:])
+        ident_f32 = keep.tile([P, P], F32)
+        make_identity(nc, ident_f32[:])
+
+        mask = {}
+        for smaller in (True, False):
+            table = keep.tile([P, P], BF16, name="mask%d" % smaller)
+            nc.vector.memset(table[:], NEG)
+            for line in range(LINES):
+                lo, hi = (0, line * SIDE) if smaller else ((line + 1) * SIDE, P)
+                if lo < hi:
+                    nc.vector.memset(table[line * SIDE : (line + 1) * SIDE, lo:hi], 0.0)
+            mask[smaller] = table
+
+        e_home = {}
+        row_sum_parts = {}
+        blind_codes = {}
+        blind_scales = {}
+        for direction in (LEFT, RIGHT):
+            smaller = sees_smaller(direction)
+            for i in range(TILES):
+                e = keep.tile([P, POSITIONS], BF16, name="e%d_%d" % (smaller, i))
+                first, behind = seen_keys(direction, i)
+                passes = pass_list(direction, i)
+                if smaller:
+                    lo, hi = behind, (passes[-1] + 1) * K_PASS
+                else:
+                    lo, hi = passes[0] * K_PASS, first
+                nc.vector.memset(e[:, lo:hi], 0.0)
+                if i == blind_tile(direction):
+                    nc.vector.memset(e[blind_rows(direction), lo:hi], 1.0)
+                e_home[(smaller, i)] = e
+            parts = keep.tile([P, TILES, PASSES], F32, name="row_sum_parts%d" % smaller)
+            nc.vector.memset(parts[:], 0.0)
+            row_sum_parts[smaller] = parts
+            ones = keep.tile([P, P, PACK], BF16, name="ones%d" % smaller, align_bytes=64)
+            nc.vector.memset(ones[:], 0.0)
+            nc.vector.memset(ones[:, blind_rows(direction), :], 1.0)
+            codes = keep.tile([P, P], U32, name="blind_codes%d" % smaller, align_bytes=64)
+            scales = keep.tile([P, P], U8, name="blind_scales%d" % smaller, align_bytes=64)
+            nc.vector.quantize_mx(
+                out=codes[:].bitcast(FP8X4),
+                scales=scales[:],
+                in_=ones[:].rearrange("p w t -> p (w t)"),
+            )
+            blind_codes[smaller] = codes
+            blind_scales[smaller] = scales
+
+        total = keep.tile([P, TILES, CHANNELS], F32)
+        out_rows = out[0].rearrange("(i p) c -> p i c", p=P)
+
+        v_grouped = {}
+        v_codes = {}
+        v_scales = {}
+        q_t = {}
+        k_t = {}
+        e_codes = {}
+        e_scales = {}
+        grouped_of = {}
+        inverse = {}
+        side_sum = {}
+        channels_first = {}
+
+        def transposed(raw, h, name):
+            bank = psum_turn.tile([P, POSITIONS], BF16, tag="turn")
+            for i in range(TILES):
+                nc.tensor.transpose(
+                    bank[:, i * P : (i + 1) * P],
+                    raw[:, i, h * WIDTH : (h + 1) * WIDTH],
+                    ident_bf16[:],
+                )
+            result = operands.tile([P, POSITIONS], BF16, name=name, tag=name)
+            nc.vector.tensor_copy(out=result[:], in_=bank[:])
+            return result
+
+        def prepare_scores(g):
+            direction, h = groups[g]
+            if sees_smaller(direction):
+                q_t[h] = transposed(q_raw[in_columns(direction)], h, "q_t")
+            k_t[g] = transposed(k_raw[direction], h, "k_t")
+
+        def regroup_values(columns):
+            by_half = (
+                v_keys_columns[:].rearrange("p b u x -> p u b x") if columns else v_keys_rows[:]
+            )
+            for b in range(PASSES):
+                v_grouped[b] = work.tile(
+                    [P, CHANNELS, HALVES, PAIR], BF16, name="v_grouped", tag="v_grouped", bufs=2, align_bytes=64
+                )
+                nc.gpsimd.tensor_scalar(
+                    out=v_grouped[b][:],
+                    in0=by_half[:, b * HALVES : (b + 1) * HALVES].rearrange("p u b x -> p x u b"),
+                    scalar1=1.0,
+                    scalar2=0.0,
+                    op0=ALU.mult,
+                    op1=ALU.add,
+                )
+
+        def quantise_values(columns):
+            codes = keep.tile([P, PASSES * CHANNELS], U32, name="v_codes%d" % columns, align_bytes=64)
+            scales = keep.tile([P, PASSES * CHANNELS], U8, name="v_scales%d" % columns, align_bytes=64)
+            for b in range(PASSES):
+                cols = slice(b * CHANNELS, (b + 1) * CHANNELS)
+                nc.vector.quantize_mx(
+                    out=codes[:, cols].bitcast(FP8X4),
+                    scales=scales[:, cols],
+                    in_=v_grouped[b][:].rearrange("p x u b -> p (x u b)"),
+                )
+            v_codes[columns] = codes
+            v_scales[columns] = scales
+
+        def scores_and_exp(g, i):
+            direction, h = groups[g]
+            smaller = sees_smaller(direction)
+            first, behind = seen_keys(direction, i)
+            own_lo, own_hi = max(first, i * P), min(behind, (i + 1) * P)
+            e = e_home[(smaller, i)]
+            banks = []
+            for b in pass_list(direction, i):
+                lo = max(first, b * K_PASS)
+                hi = min(behind, (b + 1) * K_PASS)
+                keys = slice(lo, hi)
+                cols = slice(lo - b * K_PASS, hi - b * K_PASS)
+                s_bank = psum_scores.tile([P, K_PASS], F32, tag="scores")
+                on_diagonal = lo <= own_lo < hi
+                nc.tensor.matmul(
+                    s_bank[:, cols],
+                    lhsT=q_t[h][:, i * P : (i + 1) * P],
+                    rhs=k_t[g][:, keys],
+                    start=True,
+                    stop=not on_diagonal,
+                )
+                if on_diagonal:
+                    nc.tensor.matmul(
+                        s_bank[:, own_lo - b * K_PASS : own_hi - b * K_PASS],
+                        lhsT=ident_bf16[:],
+                        rhs=mask[smaller][:, own_lo - i * P : own_hi - i * P],
+                        start=False,
+                        stop=True,
+                    )
+                banks.append((b, s_bank, cols, keys))
+
+            neg_max = work.tile([P, 1], F32)
+            if len(banks) == 1:
+                b, s_bank, cols, keys = banks[0]
+                nc.vector.tensor_reduce(
+                    out=neg_max[:], in_=s_bank[:, cols], axis=AXIS_X, op=ALU.max, negate=True
+                )
+            else:
+                bank_max = work.tile([P, PASSES], F32)
+                for b, s_bank, cols, keys in banks:
+                    nc.vector.tensor_reduce(
+                        out=bank_max[:, b : b + 1], in_=s_bank[:, cols], axis=AXIS_X, op=ALU.max
+                    )
+                nc.vector.tensor_reduce(
+                    out=neg_max[:], in_=bank_max[:], axis=AXIS_X, op=ALU.max, negate=True
+                )
+            for b, s_bank, cols, keys in banks:
+                nc.scalar.activation(
+                    out=e[:, keys],
+                    in_=s_bank[:, cols],
+                    func=ACT.Exp,
+                    bias=neg_max[:, 0:1],
+                    scale=1.0,
+                    accum_out=row_sum_parts[smaller][:, i, b : b + 1],
+                )
+            if i == blind_tile(direction):
+                nc.gpsimd.memset(e[blind_rows(direction), own_lo:own_hi], 1.0)
+
+        def turn(g, i):
+            direction, h = groups[g]
+            passes = pass_list(direction, i)
+            count = len(passes)
+            e_words = e_home[(sees_smaller(direction), i)][:].bitcast(F32)
+            e_t = psum_turn.tile([P, PASSES, HALVES, P], F32, tag="turn")
+            for n, b in enumerate(passes):
+                for u in range(HALVES):
+                    w0 = (b * HALVES + u) * P
+                    nc.tensor.transpose(e_t[:, n, u, :], e_words[:, w0 : w0 + P], ident_f32[:])
+            grouped = work.tile([P, PASSES * K_PASS], BF16, align_bytes=64)
+            nc.scalar.copy(
+                out=grouped[:]
+                .bitcast(F32)[:, 0 : count * P * HALVES]
+                .rearrange("p (n w u) -> p n w u", n=count, u=HALVES),
+                in_=e_t[:, 0:count].rearrange("p n u w -> p n w u"),
+            )
+            grouped_of[(g, i)] = grouped
+
+        def quantise(g, i):
+            direction, h = groups[g]
+            passes = pass_list(direction, i)
+            if i == TILE_ORDER[0]:
+                e_codes[g] = operands.tile(
+                    [P, TILES * PASSES * P], U32, name="e_codes", tag="e_codes", align_bytes=64
+                )
+                e_scales[g] = operands.tile(
+                    [P, TILES * PASSES * P], U8, name="e_scales", tag="e_scales", align_bytes=64
+                )
+            words = slice((i * PASSES + passes[0]) * P, (i * PASSES + passes[-1] + 1) * P)
+            nc.vector.quantize_mx(
+                out=e_codes[g][:, words].bitcast(FP8X4),
+                scales=e_scales[g][:, words],
+                in_=grouped_of[(g, i)][:, 0 : len(passes) * K_PASS],
+            )
+
+        def normalise(g):
+            direction, h = groups[g]
+            row_sum = work.tile([P, TILES], F32)
+            nc.vector.tensor_reduce(
+                out=row_sum[:], in_=row_sum_parts[sees_smaller(direction)][:], axis=AXIS_X, op=ALU.add
+            )
+            blind = blind_tile(direction)
+            nc.vector.memset(row_sum[blind_rows(direction), blind : blind + 1], float(POSITIONS))
+            inverse[g] = work.tile([P, TILES], F32, name="inverse", tag="inverse")
+            nc.vector.reciprocal(out=inverse[g][:], in_=row_sum[:])
+
+        def weighted_values(g, tiles):
+            direction, h = groups[g]
+            smaller = sees_smaller(direction)
+            columns = in_columns(direction)
+            head = slice(h * WIDTH, (h + 1) * WIDTH)
+            pv = psum_pv.tile([P, ROUND, WIDTH], F32, tag="pv")
+            for n, i in enumerate(tiles):
+                passes = pass_list(direction, i)
+                lhs = []
+                for b in passes:
+                    words = slice((i * PASSES + b) * P, (i * PASSES + b + 1) * P)
+                    lhs.append((b, e_codes[g][:, words], e_scales[g][:, words]))
+                if i == blind_tile(direction):
+                    lhs.append((PASSES - 1 - passes[0], blind_codes[smaller][:], blind_scales[smaller][:]))
+                for k, (b, codes, scales) in enumerate(lhs):
+                    of_v = slice(b * CHANNELS + h * WIDTH, b * CHANNELS + (h + 1) * WIDTH)
+                    nc.tensor.matmul_mx(
+                        out=pv[:, n, :],
+                        lhsT=codes.bitcast(FP8X4),
+                        lhsT_scale=scales,
+                        rhs=v_codes[columns][:, of_v].bitcast(FP8X4),
+                        rhs_scale=v_scales[columns][:, of_v],
+                        start=(k == 0),
+                        stop=(k == len(lhs) - 1),
+                    )
+            if direction == LEFT and tiles[0] == TILE_ORDER[0]:
+                side_sum[h] = work.tile([P, TILES, WIDTH], F32, name="side_sum", tag="side_sum", bufs=2)
+            for n, i in enumerate(tiles):
+                one_over = inverse[g][:, i : i + 1]
+                if direction == LEFT:
+                    nc.scalar.activation(
+                        out=side_sum[h][:, i, :], in_=pv[:, n, :], func=ACT.Copy, scale=one_over
+                    )
+                    continue
+                acc = side_sum[h][:, i, :] if columns else total[:, i, head]
+                nc.vector.scalar_tensor_tensor(
+                    out=acc, in0=pv[:, n, :], scalar=one_over, in1=acc, op0=ALU.mult, op1=ALU.add
+                )
+                if direction == DOWN:
+                    result = work.tile([P, WIDTH], F32)
+                    nc.gpsimd.tensor_scalar(
+                        out=result[:], in0=acc, scalar1=0.2, scalar2=0.0, op0=ALU.mult, op1=ALU.add
+                    )
+                    nc.sync.dma_start(out=out_rows[:, i, head], in_=result[:])
+
+        def to_channels(h):
+            channels_first[h] = work.tile(
+                [P, SIDE, SIDE], F32, name="channels_first", tag="channels_first", bufs=2
+            )
+            for half in range(TILES // ROUND):
+                bank = psum_turn.tile([P, ROUND * P], F32, tag="turn")
+                for n in range(ROUND):
+                    nc.tensor.transpose(
+                        bank[:, n * P : (n + 1) * P], side_sum[h][:, half * ROUND + n, :], ident_f32[:]
+                    )
+                window_columns = slice(half * ROUND * LINES, (half + 1) * ROUND * LINES)
+                nc.scalar.copy(
+                    out=channels_first[h][:, :, window_columns],
+                    in_=bank[:].rearrange("p (c r) -> p r c", r=SIDE),
+                )
+
+        def to_rows(h):
+            head = slice(h * WIDTH, (h + 1) * WIDTH)
+            flat = channels_first[h][:].rearrange("p r c -> p (r c)")
+            for half in range(TILES // ROUND):
+                bank = psum_turn.tile([P, ROUND, P], F32, tag="turn")
+                for n in range(ROUND):
+                    i = half * ROUND + n
+                    nc.tensor.transpose(bank[:, n, :], flat[:, i * P : (i + 1) * P], ident_f32[:])
+                tiles = slice(half * ROUND, (half + 1) * ROUND)
+                nc.vector.tensor_tensor(
+                    out=total[:, tiles, head], in0=bank[:], in1=v_rows[:, tiles, head], op=ALU.add
+                )
+
+        n_units = len(groups) * TILES
+        prepare_scores(0)
+        for step in range(n_units + TILES):
+            g, position = divmod(step, TILES)
+            if step < n_units:
+                scores_and_exp(g, TILE_ORDER[position])
+            if TURN_LAG <= step < n_units + TURN_LAG:
+                g_old, at = divmod(step - TURN_LAG, TILES)
+                turn(g_old, TILE_ORDER[at])
+            if QUANT_LAG <= step < n_units + QUANT_LAG:
+                g_old, at = divmod(step - QUANT_LAG, TILES)
+                quantise(g_old, TILE_ORDER[at])
+
+            if position == AT_PREPARE and g + 1 < len(groups):
+                prepare_scores(g + 1)
+            if g < len(groups) and groups[g] in ((LEFT, 0), (UP, 0)):
+                if position == AT_REGROUP_VALUES:
+                    regroup_values(in_columns(groups[g][0]))
+                if position == AT_QUANTISE_VALUES:
+                    quantise_values(in_columns(groups[g][0]))
+            if g == 0:
+                continue
+            before = g - 1
+            if position == AT_NORMALISE:
+                normalise(before)
+            if position == AT_FIRST_ROUND:
+                weighted_values(before, TILE_ORDER[:ROUND])
+            if position == AT_SECOND_ROUND:
+                weighted_values(before, TILE_ORDER[ROUND:])
+            if groups[before][0] == RIGHT and position == AT_TO_CHANNELS:
+                to_channels(groups[before][1])
+            if groups[before][0] == RIGHT and position == AT_TO_ROWS:
+                to_rows(groups[before][1])

@@ -10,7 +10,6 @@ U8 = mybir.dt.uint8
 FP8X4 = mybir.dt.float8_e4m3fn_x4
 ALU = mybir.AluOpType
 ACT = mybir.ActivationFunctionType
-AXIS_X = mybir.AxisListType.X
 
 P = 128
 SIDE = 32
@@ -34,16 +33,23 @@ FLOPS = 2 * 2 * 4 * HEADS * POSITIONS * POSITIONS * WIDTH
 TILE_ORDER = [t for a in range(TILES // 2) for t in (a, TILES - 1 - a)]
 ROUND = CHUNKS
 
-TURN_LAG = 2
-QUANT_LAG = 3
-AT_NORMALISE = 0
-AT_FIRST_ROUND = 1
+EXP_LAG = 2
+TURN_LAG = 4
+QUANT_LAG = 6
 AT_REGROUP_VALUES = 2
-AT_SECOND_ROUND = 3
-AT_TO_CHANNELS = 4
-AT_PREPARE = 5
-AT_TO_ROWS = 6
-AT_QUANTISE_VALUES = 6
+AT_TURN_INPUTS = 3
+AT_KEEP_INPUTS = 4
+AT_QUANTISE_VALUES = 7
+AT_FIRST_ROUND = 2
+AT_NORMALISE = 5
+AT_FIRST_SUM = 6
+AT_SECOND_ROUND = 7
+AT_SECOND_SUM = 9
+AT_TO_CHANNELS = 14
+AT_REORDER = 15
+AT_TO_ROWS = 17
+AT_JOIN = 18
+DRAIN = AT_SECOND_SUM + 1
 
 
 def sees_smaller(direction):
@@ -82,9 +88,10 @@ def tile_localdirectionalattention_pa_kernel(tc, q, k_dir, v, out):
         keep = ctx.enter_context(tc.tile_pool(name="keep", bufs=1))
         operands = ctx.enter_context(tc.tile_pool(name="operands", bufs=2))
         work = ctx.enter_context(tc.tile_pool(name="work", bufs=4))
-        psum_scores = ctx.enter_context(tc.psum_pool(name="psum_scores", bufs=5))
-        psum_turn = ctx.enter_context(tc.psum_pool(name="psum_turn", bufs=2))
-        psum_pv = ctx.enter_context(tc.psum_pool(name="psum_pv", bufs=1))
+        psum_scores = ctx.enter_context(tc.psum_pool(name="psum_scores", bufs=3))
+        psum_turn = ctx.enter_context(tc.psum_pool(name="psum_turn", bufs=3))
+        psum_pv = ctx.enter_context(tc.psum_pool(name="psum_pv", bufs=2))
+        ctx.enter_context(tc.manual_schedule())
 
         def load_in_columns(dst, src, h):
             head = slice(h * WIDTH, (h + 1) * WIDTH)
@@ -145,7 +152,6 @@ def tile_localdirectionalattention_pa_kernel(tc, q, k_dir, v, out):
             mask[smaller] = table
 
         e_home = {}
-        row_sum_parts = {}
         blind_codes = {}
         blind_scales = {}
         for direction in (LEFT, RIGHT):
@@ -162,9 +168,6 @@ def tile_localdirectionalattention_pa_kernel(tc, q, k_dir, v, out):
                 if i == blind_tile(direction):
                     nc.vector.memset(e[blind_rows(direction), lo:hi], 1.0)
                 e_home[(smaller, i)] = e
-            parts = keep.tile([P, TILES, PASSES], F32, name="row_sum_parts%d" % smaller)
-            nc.vector.memset(parts[:], 0.0)
-            row_sum_parts[smaller] = parts
             ones = keep.tile([P, P, PACK], BF16, name="ones%d" % smaller, align_bytes=64)
             nc.vector.memset(ones[:], 0.0)
             nc.vector.memset(ones[:, blind_rows(direction), :], 1.0)
@@ -184,8 +187,15 @@ def tile_localdirectionalattention_pa_kernel(tc, q, k_dir, v, out):
         v_grouped = {}
         v_codes = {}
         v_scales = {}
+        turned = {}
         q_t = {}
         k_t = {}
+        banks_of = {}
+        staged_of = {}
+        neg_max_of = {}
+        row_sum = {}
+        e_t_of = {}
+        pv_of = {}
         e_codes = {}
         e_scales = {}
         grouped_of = {}
@@ -193,23 +203,28 @@ def tile_localdirectionalattention_pa_kernel(tc, q, k_dir, v, out):
         side_sum = {}
         channels_first = {}
 
-        def transposed(raw, h, name):
-            bank = psum_turn.tile([P, POSITIONS], BF16, tag="turn")
-            for i in range(TILES):
-                nc.tensor.transpose(
-                    bank[:, i * P : (i + 1) * P],
-                    raw[:, i, h * WIDTH : (h + 1) * WIDTH],
-                    ident_bf16[:],
-                )
-            result = operands.tile([P, POSITIONS], BF16, name=name, tag=name)
-            nc.vector.tensor_copy(out=result[:], in_=bank[:])
-            return result
-
-        def prepare_scores(g):
+        def turn_inputs(g):
             direction, h = groups[g]
+            sources = [("k_t", k_raw[direction])]
             if sees_smaller(direction):
-                q_t[h] = transposed(q_raw[in_columns(direction)], h, "q_t")
-            k_t[g] = transposed(k_raw[direction], h, "k_t")
+                sources.append(("q_t", q_raw[in_columns(direction)]))
+            for name, raw in sources:
+                bank = psum_turn.tile([P, POSITIONS], BF16, tag="turn")
+                for i in range(TILES):
+                    nc.tensor.transpose(
+                        bank[:, i * P : (i + 1) * P],
+                        raw[:, i, h * WIDTH : (h + 1) * WIDTH],
+                        ident_bf16[:],
+                    )
+                turned[name] = bank
+
+        def keep_inputs(g):
+            direction, h = groups[g]
+            k_t[g] = operands.tile([P, POSITIONS], BF16, name="k_t", tag="k_t")
+            nc.scalar.copy(out=k_t[g][:], in_=turned["k_t"][:])
+            if sees_smaller(direction):
+                q_t[h] = operands.tile([P, POSITIONS], BF16, name="q_t", tag="q_t")
+                nc.scalar.copy(out=q_t[h][:], in_=turned["q_t"][:])
 
         def regroup_values(columns):
             by_half = (
@@ -241,24 +256,21 @@ def tile_localdirectionalattention_pa_kernel(tc, q, k_dir, v, out):
             v_codes[columns] = codes
             v_scales[columns] = scales
 
-        def scores_and_exp(g, i):
+        def scores(g, i):
             direction, h = groups[g]
             smaller = sees_smaller(direction)
             first, behind = seen_keys(direction, i)
             own_lo, own_hi = max(first, i * P), min(behind, (i + 1) * P)
-            e = e_home[(smaller, i)]
             banks = []
             for b in pass_list(direction, i):
                 lo = max(first, b * K_PASS)
                 hi = min(behind, (b + 1) * K_PASS)
-                keys = slice(lo, hi)
-                cols = slice(lo - b * K_PASS, hi - b * K_PASS)
                 s_bank = psum_scores.tile([P, K_PASS], F32, tag="scores")
                 on_diagonal = lo <= own_lo < hi
                 nc.tensor.matmul(
-                    s_bank[:, cols],
+                    s_bank[:, lo - b * K_PASS : hi - b * K_PASS],
                     lhsT=q_t[h][:, i * P : (i + 1) * P],
-                    rhs=k_t[g][:, keys],
+                    rhs=k_t[g][:, lo:hi],
                     start=True,
                     stop=not on_diagonal,
                 )
@@ -270,51 +282,61 @@ def tile_localdirectionalattention_pa_kernel(tc, q, k_dir, v, out):
                         start=False,
                         stop=True,
                     )
-                banks.append((b, s_bank, cols, keys))
+                banks.append((s_bank[:, lo - b * K_PASS : hi - b * K_PASS], lo, hi))
+            banks_of[(g, i)] = banks
 
-            neg_max = work.tile([P, 1], F32)
-            if len(banks) == 1:
-                b, s_bank, cols, keys = banks[0]
-                nc.vector.tensor_reduce(
-                    out=neg_max[:], in_=s_bank[:, cols], axis=AXIS_X, op=ALU.max, negate=True
-                )
-            else:
-                bank_max = work.tile([P, PASSES], F32)
-                for b, s_bank, cols, keys in banks:
-                    nc.vector.tensor_reduce(
-                        out=bank_max[:, b : b + 1], in_=s_bank[:, cols], axis=AXIS_X, op=ALU.max
-                    )
-                nc.vector.tensor_reduce(
-                    out=neg_max[:], in_=bank_max[:], axis=AXIS_X, op=ALU.max, negate=True
-                )
-            for b, s_bank, cols, keys in banks:
-                nc.scalar.activation(
-                    out=e[:, keys],
-                    in_=s_bank[:, cols],
-                    func=ACT.Exp,
-                    bias=neg_max[:, 0:1],
-                    scale=1.0,
-                    accum_out=row_sum_parts[smaller][:, i, b : b + 1],
-                )
+        def stage_scores(g, i, n):
+            in_psum, lo, hi = banks_of[(g, i)][n]
+            if n == 0:
+                staged_of[(g, i)] = work.tile([P, POSITIONS], F32, name="staged", tag="staged")
+            lowest = work.tile([P, 1], F32, bufs=8)
+            nc.vector.tensor_scalar(
+                out=staged_of[(g, i)][:, lo:hi],
+                in0=in_psum,
+                scalar1=-1.0,
+                scalar2=None if n == 0 else neg_max_of[(g, i)][:, 0:1],
+                op0=ALU.mult,
+                op1=ALU.min,
+                accum_out=lowest[:],
+            )
+            neg_max_of[(g, i)] = lowest
+
+        def exponential(g, i):
+            direction, h = groups[g]
+            first, behind = seen_keys(direction, i)
+            e = e_home[(sees_smaller(direction), i)]
+            if i == TILE_ORDER[0]:
+                row_sum[g] = work.tile([P, TILES], F32, name="row_sum", tag="row_sum")
+            nc.scalar.activation(
+                out=e[:, first:behind],
+                in_=staged_of[(g, i)][:, first:behind],
+                func=ACT.Exp,
+                bias=neg_max_of[(g, i)][:, 0:1],
+                scale=-1.0,
+                accum_out=row_sum[g][:, i : i + 1],
+            )
             if i == blind_tile(direction):
+                own_lo, own_hi = max(first, i * P), min(behind, (i + 1) * P)
                 nc.gpsimd.memset(e[blind_rows(direction), own_lo:own_hi], 1.0)
 
         def turn(g, i):
             direction, h = groups[g]
-            passes = pass_list(direction, i)
-            count = len(passes)
             e_words = e_home[(sees_smaller(direction), i)][:].bitcast(F32)
             e_t = psum_turn.tile([P, PASSES, HALVES, P], F32, tag="turn")
-            for n, b in enumerate(passes):
+            for n, b in enumerate(pass_list(direction, i)):
                 for u in range(HALVES):
                     w0 = (b * HALVES + u) * P
                     nc.tensor.transpose(e_t[:, n, u, :], e_words[:, w0 : w0 + P], ident_f32[:])
+            e_t_of[(g, i)] = e_t
+
+        def regroup(g, i):
+            count = len(pass_list(groups[g][0], i))
             grouped = work.tile([P, PASSES * K_PASS], BF16, align_bytes=64)
             nc.scalar.copy(
                 out=grouped[:]
                 .bitcast(F32)[:, 0 : count * P * HALVES]
                 .rearrange("p (n w u) -> p n w u", n=count, u=HALVES),
-                in_=e_t[:, 0:count].rearrange("p n u w -> p n w u"),
+                in_=e_t_of[(g, i)][:, 0:count].rearrange("p n u w -> p n w u"),
             )
             grouped_of[(g, i)] = grouped
 
@@ -337,20 +359,15 @@ def tile_localdirectionalattention_pa_kernel(tc, q, k_dir, v, out):
 
         def normalise(g):
             direction, h = groups[g]
-            row_sum = work.tile([P, TILES], F32)
-            nc.vector.tensor_reduce(
-                out=row_sum[:], in_=row_sum_parts[sees_smaller(direction)][:], axis=AXIS_X, op=ALU.add
-            )
-            blind = blind_tile(direction)
-            nc.vector.memset(row_sum[blind_rows(direction), blind : blind + 1], float(POSITIONS))
             inverse[g] = work.tile([P, TILES], F32, name="inverse", tag="inverse")
-            nc.vector.reciprocal(out=inverse[g][:], in_=row_sum[:])
+            nc.vector.reciprocal(out=inverse[g][:], in_=row_sum[g][:])
+            blind = blind_tile(direction)
+            nc.vector.memset(inverse[g][blind_rows(direction), blind : blind + 1], 1.0 / POSITIONS)
 
         def weighted_values(g, tiles):
             direction, h = groups[g]
             smaller = sees_smaller(direction)
             columns = in_columns(direction)
-            head = slice(h * WIDTH, (h + 1) * WIDTH)
             pv = psum_pv.tile([P, ROUND, WIDTH], F32, tag="pv")
             for n, i in enumerate(tiles):
                 passes = pass_list(direction, i)
@@ -371,6 +388,12 @@ def tile_localdirectionalattention_pa_kernel(tc, q, k_dir, v, out):
                         start=(k == 0),
                         stop=(k == len(lhs) - 1),
                     )
+            pv_of[(g, tiles[0])] = pv
+
+        def sum_up(g, tiles):
+            direction, h = groups[g]
+            head = slice(h * WIDTH, (h + 1) * WIDTH)
+            pv = pv_of[(g, tiles[0])]
             if direction == LEFT and tiles[0] == TILE_ORDER[0]:
                 side_sum[h] = work.tile([P, TILES, WIDTH], F32, name="side_sum", tag="side_sum", bufs=2)
             for n, i in enumerate(tiles):
@@ -380,7 +403,7 @@ def tile_localdirectionalattention_pa_kernel(tc, q, k_dir, v, out):
                         out=side_sum[h][:, i, :], in_=pv[:, n, :], func=ACT.Copy, scale=one_over
                     )
                     continue
-                acc = side_sum[h][:, i, :] if columns else total[:, i, head]
+                acc = side_sum[h][:, i, :] if in_columns(direction) else total[:, i, head]
                 nc.vector.scalar_tensor_tensor(
                     out=acc, in0=pv[:, n, :], scalar=one_over, in1=acc, op0=ALU.mult, op1=ALU.add
                 )
@@ -392,64 +415,93 @@ def tile_localdirectionalattention_pa_kernel(tc, q, k_dir, v, out):
                     nc.sync.dma_start(out=out_rows[:, i, head], in_=result[:])
 
         def to_channels(h):
-            channels_first[h] = work.tile(
-                [P, SIDE, SIDE], F32, name="channels_first", tag="channels_first", bufs=2
-            )
             for half in range(TILES // ROUND):
                 bank = psum_turn.tile([P, ROUND * P], F32, tag="turn")
                 for n in range(ROUND):
                     nc.tensor.transpose(
                         bank[:, n * P : (n + 1) * P], side_sum[h][:, half * ROUND + n, :], ident_f32[:]
                     )
+                turned[half] = bank
+
+        def reorder(h):
+            channels_first[h] = work.tile(
+                [P, SIDE, SIDE], F32, name="channels_first", tag="channels_first", bufs=2
+            )
+            for half in range(TILES // ROUND):
                 window_columns = slice(half * ROUND * LINES, (half + 1) * ROUND * LINES)
                 nc.scalar.copy(
                     out=channels_first[h][:, :, window_columns],
-                    in_=bank[:].rearrange("p (c r) -> p r c", r=SIDE),
+                    in_=turned[half][:].rearrange("p (c r) -> p r c", r=SIDE),
                 )
 
         def to_rows(h):
-            head = slice(h * WIDTH, (h + 1) * WIDTH)
             flat = channels_first[h][:].rearrange("p r c -> p (r c)")
             for half in range(TILES // ROUND):
                 bank = psum_turn.tile([P, ROUND, P], F32, tag="turn")
                 for n in range(ROUND):
                     i = half * ROUND + n
                     nc.tensor.transpose(bank[:, n, :], flat[:, i * P : (i + 1) * P], ident_f32[:])
+                turned[half] = bank
+
+        def join(h):
+            head = slice(h * WIDTH, (h + 1) * WIDTH)
+            for half in range(TILES // ROUND):
                 tiles = slice(half * ROUND, (half + 1) * ROUND)
                 nc.vector.tensor_tensor(
-                    out=total[:, tiles, head], in0=bank[:], in1=v_rows[:, tiles, head], op=ALU.add
+                    out=total[:, tiles, head], in0=turned[half][:], in1=v_rows[:, tiles, head], op=ALU.add
                 )
 
+        def unit(index):
+            g, position = divmod(index, TILES)
+            return g, TILE_ORDER[position]
+
         n_units = len(groups) * TILES
-        prepare_scores(0)
-        for step in range(n_units + TILES):
+        turn_inputs(0)
+        keep_inputs(0)
+        for step in range(n_units + DRAIN):
             g, position = divmod(step, TILES)
             if step < n_units:
-                scores_and_exp(g, TILE_ORDER[position])
+                scores(*unit(step))
+                stage_scores(*unit(step), 0)
             if TURN_LAG <= step < n_units + TURN_LAG:
-                g_old, at = divmod(step - TURN_LAG, TILES)
-                turn(g_old, TILE_ORDER[at])
+                turn(*unit(step - TURN_LAG))
+            if EXP_LAG <= step < n_units + EXP_LAG:
+                exponential(*unit(step - EXP_LAG))
+            if TURN_LAG <= step < n_units + TURN_LAG:
+                regroup(*unit(step - TURN_LAG))
             if QUANT_LAG <= step < n_units + QUANT_LAG:
-                g_old, at = divmod(step - QUANT_LAG, TILES)
-                quantise(g_old, TILE_ORDER[at])
+                quantise(*unit(step - QUANT_LAG))
+            if step < n_units and len(banks_of[unit(step)]) == PASSES:
+                stage_scores(*unit(step), 1)
 
-            if position == AT_PREPARE and g + 1 < len(groups):
-                prepare_scores(g + 1)
+            if g + 1 < len(groups):
+                if position == AT_TURN_INPUTS:
+                    turn_inputs(g + 1)
+                if position == AT_KEEP_INPUTS:
+                    keep_inputs(g + 1)
             if g < len(groups) and groups[g] in ((LEFT, 0), (UP, 0)):
                 if position == AT_REGROUP_VALUES:
                     regroup_values(in_columns(groups[g][0]))
                 if position == AT_QUANTISE_VALUES:
                     quantise_values(in_columns(groups[g][0]))
-            if g == 0:
-                continue
-            before = g - 1
-            if position == AT_NORMALISE:
-                normalise(before)
-            if position == AT_FIRST_ROUND:
-                weighted_values(before, TILE_ORDER[:ROUND])
-            if position == AT_SECOND_ROUND:
-                weighted_values(before, TILE_ORDER[ROUND:])
-            if groups[before][0] == RIGHT and position == AT_TO_CHANNELS:
-                to_channels(groups[before][1])
-            if groups[before][0] == RIGHT and position == AT_TO_ROWS:
-                to_rows(groups[before][1])
+            for ended in range(max(0, g - 3), min(g, len(groups))):
+                since = step - (ended + 1) * TILES
+                direction, h = groups[ended]
+                if since == AT_FIRST_ROUND:
+                    weighted_values(ended, TILE_ORDER[:ROUND])
+                if since == AT_NORMALISE:
+                    normalise(ended)
+                if since == AT_FIRST_SUM:
+                    sum_up(ended, TILE_ORDER[:ROUND])
+                if since == AT_SECOND_ROUND:
+                    weighted_values(ended, TILE_ORDER[ROUND:])
+                if since == AT_SECOND_SUM:
+                    sum_up(ended, TILE_ORDER[ROUND:])
+                if direction == RIGHT and since == AT_TO_CHANNELS:
+                    to_channels(h)
+                if direction == RIGHT and since == AT_REORDER:
+                    reorder(h)
+                if direction == RIGHT and since == AT_TO_ROWS:
+                    to_rows(h)
+                if direction == RIGHT and since == AT_JOIN:
+                    join(h)

@@ -221,10 +221,10 @@ def tile_localdirectionalattention_pa_kernel(tc, q, k_dir, v, out):
         def keep_inputs(g):
             direction, h = groups[g]
             k_t[g] = operands.tile([P, POSITIONS], BF16, name="k_t", tag="k_t")
-            nc.scalar.copy(out=k_t[g][:], in_=turned["k_t"][:])
+            nc.vector.tensor_copy(out=k_t[g][:], in_=turned["k_t"][:])
             if sees_smaller(direction):
                 q_t[h] = operands.tile([P, POSITIONS], BF16, name="q_t", tag="q_t")
-                nc.scalar.copy(out=q_t[h][:], in_=turned["q_t"][:])
+                nc.vector.tensor_copy(out=q_t[h][:], in_=turned["q_t"][:])
 
         def regroup_values(columns):
             by_half = (

@@ -33,22 +33,23 @@ FLOPS = 2 * 2 * 4 * HEADS * POSITIONS * POSITIONS * WIDTH
 TILE_ORDER = [t for a in range(TILES // 2) for t in (a, TILES - 1 - a)]
 ROUND = CHUNKS
 
+SCORE_LEAD = 1
 EXP_LAG = 2
-TURN_LAG = 4
-QUANT_LAG = 6
+TURN_LAG = 5
+QUANT_LAG = 7
+AT_TURN_INPUTS = 2
 AT_REGROUP_VALUES = 2
-AT_TURN_INPUTS = 3
-AT_KEEP_INPUTS = 4
+AT_KEEP_INPUTS = 3
 AT_QUANTISE_VALUES = 7
-AT_FIRST_ROUND = 2
-AT_NORMALISE = 5
-AT_FIRST_SUM = 6
-AT_SECOND_ROUND = 7
-AT_SECOND_SUM = 9
-AT_TO_CHANNELS = 14
-AT_REORDER = 15
-AT_TO_ROWS = 17
-AT_JOIN = 18
+AT_FIRST_ROUND = 3
+AT_NORMALISE = 4
+AT_FIRST_SUM = 5
+AT_SECOND_ROUND = 8
+AT_SECOND_SUM = 10
+AT_TO_CHANNELS = 15
+AT_REORDER = 16
+AT_TO_ROWS = 18
+AT_JOIN = 19
 DRAIN = AT_SECOND_SUM + 1
 
 
@@ -89,8 +90,8 @@ def tile_localdirectionalattention_pa_kernel(tc, q, k_dir, v, out):
         operands = ctx.enter_context(tc.tile_pool(name="operands", bufs=2))
         work = ctx.enter_context(tc.tile_pool(name="work", bufs=4))
         psum_scores = ctx.enter_context(tc.psum_pool(name="psum_scores", bufs=3))
-        psum_turn = ctx.enter_context(tc.psum_pool(name="psum_turn", bufs=3))
-        psum_pv = ctx.enter_context(tc.psum_pool(name="psum_pv", bufs=2))
+        psum_turn = ctx.enter_context(tc.psum_pool(name="psum_turn", bufs=4))
+        psum_pv = ctx.enter_context(tc.psum_pool(name="psum_pv", bufs=1))
         ctx.enter_context(tc.manual_schedule())
 
         def load_in_columns(dst, src, h):
@@ -221,10 +222,10 @@ def tile_localdirectionalattention_pa_kernel(tc, q, k_dir, v, out):
         def keep_inputs(g):
             direction, h = groups[g]
             k_t[g] = operands.tile([P, POSITIONS], BF16, name="k_t", tag="k_t")
-            nc.vector.tensor_copy(out=k_t[g][:], in_=turned["k_t"][:])
+            nc.scalar.copy(out=k_t[g][:], in_=turned["k_t"][:])
             if sees_smaller(direction):
                 q_t[h] = operands.tile([P, POSITIONS], BF16, name="q_t", tag="q_t")
-                nc.vector.tensor_copy(out=q_t[h][:], in_=turned["q_t"][:])
+                nc.scalar.copy(out=q_t[h][:], in_=turned["q_t"][:])
 
         def regroup_values(columns):
             by_half = (
@@ -268,9 +269,9 @@ def tile_localdirectionalattention_pa_kernel(tc, q, k_dir, v, out):
                 s_bank = psum_scores.tile([P, K_PASS], F32, tag="scores")
                 on_diagonal = lo <= own_lo < hi
                 nc.tensor.matmul(
-                    s_bank[:, lo - b * K_PASS : hi - b * K_PASS],
+                    s_bank[:],
                     lhsT=q_t[h][:, i * P : (i + 1) * P],
-                    rhs=k_t[g][:, lo:hi],
+                    rhs=k_t[g][:, b * K_PASS : (b + 1) * K_PASS],
                     start=True,
                     stop=not on_diagonal,
                 )
@@ -288,7 +289,7 @@ def tile_localdirectionalattention_pa_kernel(tc, q, k_dir, v, out):
         def stage_scores(g, i, n):
             in_psum, lo, hi = banks_of[(g, i)][n]
             if n == 0:
-                staged_of[(g, i)] = work.tile([P, POSITIONS], F32, name="staged", tag="staged")
+                staged_of[(g, i)] = work.tile([P, POSITIONS], F32, name="staged", tag="staged", bufs=6)
             lowest = work.tile([P, 1], F32, bufs=8)
             nc.vector.tensor_scalar(
                 out=staged_of[(g, i)][:, lo:hi],
@@ -458,10 +459,13 @@ def tile_localdirectionalattention_pa_kernel(tc, q, k_dir, v, out):
         n_units = len(groups) * TILES
         turn_inputs(0)
         keep_inputs(0)
+        for ahead in range(SCORE_LEAD):
+            scores(*unit(ahead))
         for step in range(n_units + DRAIN):
             g, position = divmod(step, TILES)
+            if step + SCORE_LEAD < n_units:
+                scores(*unit(step + SCORE_LEAD))
             if step < n_units:
-                scores(*unit(step))
                 stage_scores(*unit(step), 0)
             if TURN_LAG <= step < n_units + TURN_LAG:
                 turn(*unit(step - TURN_LAG))

@@ -46,10 +46,8 @@ AT_NORMALISE = 4
 AT_FIRST_SUM = 5
 AT_SECOND_ROUND = 8
 AT_SECOND_SUM = 10
-AT_TO_CHANNELS = 15
-AT_REORDER = 16
-AT_TO_ROWS = 18
-AT_JOIN = 19
+AT_PARK = 11
+AT_FETCH = 19
 DRAIN = AT_SECOND_SUM + 1
 
 
@@ -113,7 +111,7 @@ def tile_localdirectionalattention_pa_kernel(tc, q, k_dir, v, out):
             k_raw[direction] = keep.tile([P, TILES, CHANNELS], BF16, name="k_raw%d" % direction)
         v_keys_rows = keep.tile([P, PASSES * HALVES, PAIR, CHANNELS], BF16)
         v_keys_columns = keep.tile([P, PAIR, PASSES * HALVES, CHANNELS], BF16)
-        v_rows = keep.tile([P, TILES, CHANNELS], BF16)
+        v_columns = keep.tile([P, TILES, CHANNELS], BF16)
 
         by_column = v[0].rearrange(
             "(r b u c) h d -> c r (b u) (h d)", r=SIDE // PAIR, b=PAIR, u=PASSES * HALVES, c=8
@@ -128,9 +126,13 @@ def tile_localdirectionalattention_pa_kernel(tc, q, k_dir, v, out):
                         out=v_keys_columns[c * 16 : (c + 1) * 16].rearrange("p b u x -> p (b u) x"),
                         in_=by_column[c],
                     )
+                for line in range(LINES):
+                    nc.sync.dma_start(
+                        out=v_columns[line * SIDE : (line + 1) * SIDE],
+                        in_=v[0].rearrange("(r i l) h d -> l r i (h d)", r=SIDE, i=TILES, l=LINES)[line],
+                    )
         load_in_rows(q_raw[False], q[0])
         load_in_rows(k_raw[UP], k_dir[UP, 0])
-        load_in_rows(v_rows, v[0])
         nc.sync.dma_start(
             out=v_keys_rows[:].rearrange("p u b x -> p u (b x)"),
             in_=v[0].rearrange("(u p b) h d -> p u (b h d)", p=P, b=PAIR),
@@ -202,7 +204,6 @@ def tile_localdirectionalattention_pa_kernel(tc, q, k_dir, v, out):
         grouped_of = {}
         inverse = {}
         side_sum = {}
-        channels_first = {}
 
         def turn_inputs(g):
             direction, h = groups[g]
@@ -399,14 +400,10 @@ def tile_localdirectionalattention_pa_kernel(tc, q, k_dir, v, out):
                 side_sum[h] = work.tile([P, TILES, WIDTH], F32, name="side_sum", tag="side_sum", bufs=2)
             for n, i in enumerate(tiles):
                 one_over = inverse[g][:, i : i + 1]
-                if direction == LEFT:
-                    nc.scalar.activation(
-                        out=side_sum[h][:, i, :], in_=pv[:, n, :], func=ACT.Copy, scale=one_over
-                    )
-                    continue
                 acc = side_sum[h][:, i, :] if in_columns(direction) else total[:, i, head]
+                so_far = v_columns[:, i, head] if direction == LEFT else acc
                 nc.vector.scalar_tensor_tensor(
-                    out=acc, in0=pv[:, n, :], scalar=one_over, in1=acc, op0=ALU.mult, op1=ALU.add
+                    out=acc, in0=pv[:, n, :], scalar=one_over, in1=so_far, op0=ALU.mult, op1=ALU.add
                 )
                 if direction == DOWN:
                     result = work.tile([P, WIDTH], F32)
@@ -415,42 +412,17 @@ def tile_localdirectionalattention_pa_kernel(tc, q, k_dir, v, out):
                     )
                     nc.sync.dma_start(out=out_rows[:, i, head], in_=result[:])
 
-        def to_channels(h):
-            for half in range(TILES // ROUND):
-                bank = psum_turn.tile([P, ROUND * P], F32, tag="turn")
-                for n in range(ROUND):
-                    nc.tensor.transpose(
-                        bank[:, n * P : (n + 1) * P], side_sum[h][:, half * ROUND + n, :], ident_f32[:]
-                    )
-                turned[half] = bank
-
-        def reorder(h):
-            channels_first[h] = work.tile(
-                [P, SIDE, SIDE], F32, name="channels_first", tag="channels_first", bufs=2
-            )
-            for half in range(TILES // ROUND):
-                window_columns = slice(half * ROUND * LINES, (half + 1) * ROUND * LINES)
-                nc.scalar.copy(
-                    out=channels_first[h][:, :, window_columns],
-                    in_=turned[half][:].rearrange("p (c r) -> p r c", r=SIDE),
-                )
-
-        def to_rows(h):
-            flat = channels_first[h][:].rearrange("p r c -> p (r c)")
-            for half in range(TILES // ROUND):
-                bank = psum_turn.tile([P, ROUND, P], F32, tag="turn")
-                for n in range(ROUND):
-                    i = half * ROUND + n
-                    nc.tensor.transpose(bank[:, n, :], flat[:, i * P : (i + 1) * P], ident_f32[:])
-                turned[half] = bank
-
-        def join(h):
+        def park(h):
             head = slice(h * WIDTH, (h + 1) * WIDTH)
-            for half in range(TILES // ROUND):
-                tiles = slice(half * ROUND, (half + 1) * ROUND)
-                nc.vector.tensor_tensor(
-                    out=total[:, tiles, head], in0=turned[half][:], in1=v_rows[:, tiles, head], op=ALU.add
+            by_line = out[0].rearrange("(r i l) c -> l r i c", r=SIDE, i=TILES, l=LINES)
+            for line in range(LINES):
+                nc.sync.dma_start(
+                    out=by_line[line][:, :, head], in_=side_sum[h][line * SIDE : (line + 1) * SIDE]
                 )
+
+        def fetch(h):
+            head = slice(h * WIDTH, (h + 1) * WIDTH)
+            nc.sync.dma_start(out=total[:, :, head], in_=out_rows[:, :, head])
 
         def unit(index):
             g, position = divmod(index, TILES)
@@ -501,11 +473,7 @@ def tile_localdirectionalattention_pa_kernel(tc, q, k_dir, v, out):
                     weighted_values(ended, TILE_ORDER[ROUND:])
                 if since == AT_SECOND_SUM:
                     sum_up(ended, TILE_ORDER[ROUND:])
-                if direction == RIGHT and since == AT_TO_CHANNELS:
-                    to_channels(h)
-                if direction == RIGHT and since == AT_REORDER:
-                    reorder(h)
-                if direction == RIGHT and since == AT_TO_ROWS:
-                    to_rows(h)
-                if direction == RIGHT and since == AT_JOIN:
-                    join(h)
+                if direction == RIGHT and since == AT_PARK:
+                    park(h)
+                if direction == RIGHT and since == AT_FETCH:
+                    fetch(h)

@@ -41,6 +41,7 @@ AT_TURN_INPUTS = 2
 AT_REGROUP_VALUES = 2
 AT_KEEP_INPUTS = 3
 AT_QUANTISE_VALUES = 7
+AT_PREPARE_SUMS = 2
 AT_FIRST_ROUND = 3
 AT_NORMALISE = 4
 AT_FIRST_SUM = 5
@@ -48,6 +49,8 @@ AT_SECOND_ROUND = 8
 AT_SECOND_SUM = 10
 AT_PARK = 11
 AT_FETCH = 19
+AT_FIFTH = 23
+AT_REORDER_QUERIES = 6
 DRAIN = AT_SECOND_SUM + 1
 
 
@@ -78,10 +81,20 @@ def blind_rows(direction):
     return slice(0, SIDE) if sees_smaller(direction) else slice(P - SIDE, P)
 
 
+def runs(tiles):
+    spans = []
+    for i in sorted(tiles):
+        if spans and spans[-1][1] == i:
+            spans[-1] = (spans[-1][0], i + 1)
+        else:
+            spans.append((i, i + 1))
+    return spans
+
+
 def tile_localdirectionalattention_pa_kernel(tc, q, k_dir, v, out):
     nc = tc.nc
-    groups = [(d, h) for h in range(HEADS) for d in (LEFT, RIGHT)]
-    groups += [(d, h) for h in range(HEADS) for d in (UP, DOWN)]
+    groups = [(d, h) for h in range(HEADS) for d in (UP, DOWN)]
+    groups += [(d, h) for h in range(HEADS) for d in (LEFT, RIGHT)]
 
     with ExitStack() as ctx:
         keep = ctx.enter_context(tc.tile_pool(name="keep", bufs=1))
@@ -92,52 +105,47 @@ def tile_localdirectionalattention_pa_kernel(tc, q, k_dir, v, out):
         psum_pv = ctx.enter_context(tc.psum_pool(name="psum_pv", bufs=1))
         ctx.enter_context(tc.manual_schedule())
 
-        def load_in_columns(dst, src, h):
-            head = slice(h * WIDTH, (h + 1) * WIDTH)
+        def load_in_rows(dst, src, heads):
+            cols = slice(heads[0] * WIDTH, (heads[-1] + 1) * WIDTH)
+            nc.sync.dma_start(
+                out=dst[:, :, cols], in_=src.rearrange("(i p) h d -> p i (h d)", p=P)[:, :, cols]
+            )
+
+        def load_in_columns(dst, src):
             by_line = src.rearrange("(r i l) h d -> l r i (h d)", r=SIDE, i=TILES, l=LINES)
             for line in range(LINES):
-                nc.sync.dma_start(
-                    out=dst[line * SIDE : (line + 1) * SIDE, :, head], in_=by_line[line][:, :, head]
-                )
+                nc.sync.dma_start(out=dst[line * SIDE : (line + 1) * SIDE], in_=by_line[line])
 
-        def load_in_rows(dst, src):
-            nc.sync.dma_start(out=dst[:], in_=src.rearrange("(i p) h d -> p i (h d)", p=P))
-
-        q_raw = {}
+        q_raw = keep.tile([P, TILES, CHANNELS], BF16)
         k_raw = {}
-        for columns in (True, False):
-            q_raw[columns] = keep.tile([P, TILES, CHANNELS], BF16, name="q_raw%d" % columns)
         for direction in (LEFT, RIGHT, UP, DOWN):
             k_raw[direction] = keep.tile([P, TILES, CHANNELS], BF16, name="k_raw%d" % direction)
         v_keys_rows = keep.tile([P, PASSES * HALVES, PAIR, CHANNELS], BF16)
         v_keys_columns = keep.tile([P, PAIR, PASSES * HALVES, CHANNELS], BF16)
-        v_columns = keep.tile([P, TILES, CHANNELS], BF16)
+        v_rows = keep.tile([P, TILES, CHANNELS], BF16)
 
-        by_column = v[0].rearrange(
-            "(r b u c) h d -> c r (b u) (h d)", r=SIDE // PAIR, b=PAIR, u=PASSES * HALVES, c=8
-        )
-        for h in range(HEADS):
-            load_in_columns(q_raw[True], q[0], h)
-            load_in_columns(k_raw[LEFT], k_dir[LEFT, 0], h)
-            load_in_columns(k_raw[RIGHT], k_dir[RIGHT, 0], h)
-            if h == 0:
-                for c in range(8):
-                    nc.sync.dma_start(
-                        out=v_keys_columns[c * 16 : (c + 1) * 16].rearrange("p b u x -> p (b u) x"),
-                        in_=by_column[c],
-                    )
-                for line in range(LINES):
-                    nc.sync.dma_start(
-                        out=v_columns[line * SIDE : (line + 1) * SIDE],
-                        in_=v[0].rearrange("(r i l) h d -> l r i (h d)", r=SIDE, i=TILES, l=LINES)[line],
-                    )
-        load_in_rows(q_raw[False], q[0])
-        load_in_rows(k_raw[UP], k_dir[UP, 0])
+        first_head, other_heads = [0], list(range(1, HEADS))
+        load_in_rows(q_raw, q[0], first_head)
+        load_in_rows(k_raw[UP], k_dir[UP, 0], first_head)
+        load_in_rows(k_raw[DOWN], k_dir[DOWN, 0], first_head)
         nc.sync.dma_start(
             out=v_keys_rows[:].rearrange("p u b x -> p u (b x)"),
             in_=v[0].rearrange("(u p b) h d -> p u (b h d)", p=P, b=PAIR),
         )
-        load_in_rows(k_raw[DOWN], k_dir[DOWN, 0])
+        load_in_rows(v_rows, v[0], first_head + other_heads)
+        load_in_rows(q_raw, q[0], other_heads)
+        load_in_rows(k_raw[UP], k_dir[UP, 0], other_heads)
+        load_in_rows(k_raw[DOWN], k_dir[DOWN, 0], other_heads)
+        load_in_columns(k_raw[LEFT], k_dir[LEFT, 0])
+        load_in_columns(k_raw[RIGHT], k_dir[RIGHT, 0])
+        by_column = v[0].rearrange(
+            "(r b u c) h d -> c r (b u) (h d)", r=SIDE // PAIR, b=PAIR, u=PASSES * HALVES, c=8
+        )
+        for c in range(8):
+            nc.sync.dma_start(
+                out=v_keys_columns[c * 16 : (c + 1) * 16].rearrange("p b u x -> p (b u) x"),
+                in_=by_column[c],
+            )
 
         ident_bf16 = keep.tile([P, P], BF16)
         make_identity(nc, ident_bf16[:])
@@ -157,7 +165,7 @@ def tile_localdirectionalattention_pa_kernel(tc, q, k_dir, v, out):
         e_home = {}
         blind_codes = {}
         blind_scales = {}
-        for direction in (LEFT, RIGHT):
+        for direction in (UP, DOWN):
             smaller = sees_smaller(direction)
             for i in range(TILES):
                 e = keep.tile([P, POSITIONS], BF16, name="e%d_%d" % (smaller, i))
@@ -167,9 +175,9 @@ def tile_localdirectionalattention_pa_kernel(tc, q, k_dir, v, out):
                     lo, hi = behind, (passes[-1] + 1) * K_PASS
                 else:
                     lo, hi = passes[0] * K_PASS, first
-                nc.vector.memset(e[:, lo:hi], 0.0)
+                nc.gpsimd.memset(e[:, lo:hi], 0.0)
                 if i == blind_tile(direction):
-                    nc.vector.memset(e[blind_rows(direction), lo:hi], 1.0)
+                    nc.gpsimd.memset(e[blind_rows(direction), lo:hi], 1.0)
                 e_home[(smaller, i)] = e
             ones = keep.tile([P, P, PACK], BF16, name="ones%d" % smaller, align_bytes=64)
             nc.vector.memset(ones[:], 0.0)
@@ -186,6 +194,7 @@ def tile_localdirectionalattention_pa_kernel(tc, q, k_dir, v, out):
 
         total = keep.tile([P, TILES, CHANNELS], F32)
         out_rows = out[0].rearrange("(i p) c -> p i c", p=P)
+        out_columns = out[0].rearrange("(r i l) c -> l r i c", r=SIDE, i=TILES, l=LINES)
 
         v_grouped = {}
         v_codes = {}
@@ -197,6 +206,7 @@ def tile_localdirectionalattention_pa_kernel(tc, q, k_dir, v, out):
         staged_of = {}
         neg_max_of = {}
         row_sum = {}
+        divisor = {}
         e_t_of = {}
         pv_of = {}
         e_codes = {}
@@ -208,8 +218,8 @@ def tile_localdirectionalattention_pa_kernel(tc, q, k_dir, v, out):
         def turn_inputs(g):
             direction, h = groups[g]
             sources = [("k_t", k_raw[direction])]
-            if sees_smaller(direction):
-                sources.append(("q_t", q_raw[in_columns(direction)]))
+            if direction == UP:
+                sources.append(("q_t", q_raw))
             for name, raw in sources:
                 bank = psum_turn.tile([P, POSITIONS], BF16, tag="turn")
                 for i in range(TILES):
@@ -224,9 +234,23 @@ def tile_localdirectionalattention_pa_kernel(tc, q, k_dir, v, out):
             direction, h = groups[g]
             k_t[g] = operands.tile([P, POSITIONS], BF16, name="k_t", tag="k_t")
             nc.scalar.copy(out=k_t[g][:], in_=turned["k_t"][:])
-            if sees_smaller(direction):
-                q_t[h] = operands.tile([P, POSITIONS], BF16, name="q_t", tag="q_t")
-                nc.scalar.copy(out=q_t[h][:], in_=turned["q_t"][:])
+            if direction == UP:
+                q_t[(False, h)] = operands.tile([P, POSITIONS], BF16, name="q_t", tag="q_t")
+                if g == 0:
+                    nc.vector.tensor_copy(out=q_t[(False, h)][:], in_=turned["q_t"][:])
+                else:
+                    nc.scalar.copy(out=q_t[(False, h)][:], in_=turned["q_t"][:])
+
+        def reorder_queries(h):
+            q_t[(True, h)] = keep.tile([P, POSITIONS], BF16, name="q_columns%d" % h)
+            nc.gpsimd.tensor_scalar(
+                out=q_t[(True, h)][:].rearrange("p (c r) -> p c r", r=SIDE),
+                in0=q_t[(False, h)][:].rearrange("p (r c) -> p c r", c=SIDE),
+                scalar1=1.0,
+                scalar2=0.0,
+                op0=ALU.mult,
+                op1=ALU.add,
+            )
 
         def regroup_values(columns):
             by_half = (
@@ -271,7 +295,7 @@ def tile_localdirectionalattention_pa_kernel(tc, q, k_dir, v, out):
                 on_diagonal = lo <= own_lo < hi
                 nc.tensor.matmul(
                     s_bank[:],
-                    lhsT=q_t[h][:, i * P : (i + 1) * P],
+                    lhsT=q_t[(in_columns(direction), h)][:, i * P : (i + 1) * P],
                     rhs=k_t[g][:, b * K_PASS : (b + 1) * K_PASS],
                     start=True,
                     stop=not on_diagonal,
@@ -359,12 +383,20 @@ def tile_localdirectionalattention_pa_kernel(tc, q, k_dir, v, out):
                 in_=grouped_of[(g, i)][:, 0 : len(passes) * K_PASS],
             )
 
-        def normalise(g):
+        def prepare_sums(g):
             direction, h = groups[g]
-            inverse[g] = work.tile([P, TILES], F32, name="inverse", tag="inverse")
-            nc.vector.reciprocal(out=inverse[g][:], in_=row_sum[g][:])
             blind = blind_tile(direction)
-            nc.vector.memset(inverse[g][blind_rows(direction), blind : blind + 1], 1.0 / POSITIONS)
+            nc.gpsimd.memset(row_sum[g][blind_rows(direction), blind : blind + 1], float(POSITIONS))
+            divisor[g] = row_sum[g]
+            if in_columns(direction):
+                divisor[g] = work.tile([P, TILES], F32, name="divisor", tag="divisor")
+                nc.gpsimd.tensor_scalar(
+                    out=divisor[g][:], in0=row_sum[g][:], scalar1=5.0, scalar2=0.0, op0=ALU.mult, op1=ALU.add
+                )
+
+        def normalise(g):
+            inverse[g] = work.tile([P, TILES], F32, name="inverse", tag="inverse")
+            nc.vector.reciprocal(out=inverse[g][:], in_=divisor[g][:])
 
         def weighted_values(g, tiles):
             direction, h = groups[g]
@@ -396,33 +428,43 @@ def tile_localdirectionalattention_pa_kernel(tc, q, k_dir, v, out):
             direction, h = groups[g]
             head = slice(h * WIDTH, (h + 1) * WIDTH)
             pv = pv_of[(g, tiles[0])]
-            if direction == LEFT and tiles[0] == TILE_ORDER[0]:
+            if direction == UP and tiles[0] == TILE_ORDER[0]:
                 side_sum[h] = work.tile([P, TILES, WIDTH], F32, name="side_sum", tag="side_sum", bufs=2)
             for n, i in enumerate(tiles):
-                one_over = inverse[g][:, i : i + 1]
-                acc = side_sum[h][:, i, :] if in_columns(direction) else total[:, i, head]
-                so_far = v_columns[:, i, head] if direction == LEFT else acc
+                acc = total[:, i, head] if in_columns(direction) else side_sum[h][:, i, :]
+                so_far = v_rows[:, i, head] if direction == UP else acc
                 nc.vector.scalar_tensor_tensor(
-                    out=acc, in0=pv[:, n, :], scalar=one_over, in1=so_far, op0=ALU.mult, op1=ALU.add
+                    out=acc,
+                    in0=pv[:, n, :],
+                    scalar=inverse[g][:, i : i + 1],
+                    in1=so_far,
+                    op0=ALU.mult,
+                    op1=ALU.add,
                 )
-                if direction == DOWN:
-                    result = work.tile([P, WIDTH], F32)
-                    nc.gpsimd.tensor_scalar(
-                        out=result[:], in0=acc, scalar1=0.2, scalar2=0.0, op0=ALU.mult, op1=ALU.add
-                    )
-                    nc.sync.dma_start(out=out_rows[:, i, head], in_=result[:])
+            if direction == RIGHT:
+                for first, behind in runs(tiles):
+                    for line in range(LINES):
+                        nc.sync.dma_start(
+                            out=out_columns[line][:, first:behind, head],
+                            in_=total[line * SIDE : (line + 1) * SIDE, first:behind, head],
+                        )
 
         def park(h):
             head = slice(h * WIDTH, (h + 1) * WIDTH)
-            by_line = out[0].rearrange("(r i l) c -> l r i c", r=SIDE, i=TILES, l=LINES)
-            for line in range(LINES):
-                nc.sync.dma_start(
-                    out=by_line[line][:, :, head], in_=side_sum[h][line * SIDE : (line + 1) * SIDE]
-                )
+            nc.sync.dma_start(out=out_rows[:, :, head], in_=side_sum[h][:])
 
         def fetch(h):
             head = slice(h * WIDTH, (h + 1) * WIDTH)
-            nc.sync.dma_start(out=total[:, :, head], in_=out_rows[:, :, head])
+            for line in range(LINES):
+                nc.sync.dma_start(
+                    out=total[line * SIDE : (line + 1) * SIDE, :, head], in_=out_columns[line][:, :, head]
+                )
+
+        def take_fifth(h):
+            head = slice(h * WIDTH, (h + 1) * WIDTH)
+            nc.gpsimd.tensor_scalar(
+                out=total[:, :, head], in0=total[:, :, head], scalar1=0.2, scalar2=0.0, op0=ALU.mult, op1=ALU.add
+            )
 
         def unit(index):
             g, position = divmod(index, TILES)
@@ -455,6 +497,8 @@ def tile_localdirectionalattention_pa_kernel(tc, q, k_dir, v, out):
                     turn_inputs(g + 1)
                 if position == AT_KEEP_INPUTS:
                     keep_inputs(g + 1)
+            if g < len(groups) and groups[g][0] == UP and position == AT_REORDER_QUERIES:
+                reorder_queries(groups[g][1])
             if g < len(groups) and groups[g] in ((LEFT, 0), (UP, 0)):
                 if position == AT_REGROUP_VALUES:
                     regroup_values(in_columns(groups[g][0]))
@@ -463,6 +507,8 @@ def tile_localdirectionalattention_pa_kernel(tc, q, k_dir, v, out):
             for ended in range(max(0, g - 3), min(g, len(groups))):
                 since = step - (ended + 1) * TILES
                 direction, h = groups[ended]
+                if since == AT_PREPARE_SUMS:
+                    prepare_sums(ended)
                 if since == AT_FIRST_ROUND:
                     weighted_values(ended, TILE_ORDER[:ROUND])
                 if since == AT_NORMALISE:
@@ -473,7 +519,9 @@ def tile_localdirectionalattention_pa_kernel(tc, q, k_dir, v, out):
                     weighted_values(ended, TILE_ORDER[ROUND:])
                 if since == AT_SECOND_SUM:
                     sum_up(ended, TILE_ORDER[ROUND:])
-                if direction == RIGHT and since == AT_PARK:
+                if direction == DOWN and since == AT_PARK:
                     park(h)
-                if direction == RIGHT and since == AT_FETCH:
+                if direction == DOWN and since == AT_FETCH:
                     fetch(h)
+                if direction == DOWN and since == AT_FIFTH:
+                    take_fifth(h)

@@ -30,28 +30,36 @@ NEG = -1.0e9
 LEFT, RIGHT, UP, DOWN = 0, 1, 2, 3
 FLOPS = 2 * 2 * 4 * HEADS * POSITIONS * POSITIONS * WIDTH
 
-TILE_ORDER = [t for a in range(TILES // 2) for t in (a, TILES - 1 - a)]
 ROUND = CHUNKS
 
-SCORE_LEAD = 1
-EXP_LAG = 2
-TURN_LAG = 5
-QUANT_LAG = 7
-AT_TURN_INPUTS = 2
-AT_REGROUP_VALUES = 2
-AT_KEEP_INPUTS = 3
-AT_QUANTISE_VALUES = 7
-AT_PREPARE_SUMS = 2
-AT_FIRST_ROUND = 3
-AT_NORMALISE = 4
-AT_FIRST_SUM = 5
-AT_SECOND_ROUND = 8
-AT_SECOND_SUM = 10
-AT_PARK = 11
-AT_FETCH = 19
-AT_FIFTH = 23
-AT_REORDER_QUERIES = 6
+SCORE_LEAD = 2
+EXP_LAG = 3
+TURN_LAG = 8
+QUANT_LAG = 13
+GROUP_SLOTS = TILES // 2 * (1 + PASSES)
+AT_TURN_KEYS = 1
+AT_KEEP_KEYS = 3
+AT_TURN_QUERIES = 4
+AT_KEEP_QUERIES = 6
+AT_QUANTISE_VALUES = 10
+AT_PREPARE_SUMS = 4
+AT_NORMALISE = 6
+AT_FIRST_ROUND = 7
+AT_FIRST_SUM = 10
+AT_SECOND_ROUND = 13
+AT_SECOND_SUM = 16
+AT_PARK = 17
+AT_FETCH = 29
+AT_FIFTH = 35
+FIFTH_TILES = 2
 DRAIN = AT_SECOND_SUM + 1
+
+
+def tile_order(direction):
+    order = []
+    for a in range(TILES // 2):
+        order += [a, TILES - 1 - a] if sees_smaller(direction) else [TILES - 1 - a, a]
+    return order
 
 
 def sees_smaller(direction):
@@ -116,7 +124,9 @@ def tile_localdirectionalattention_pa_kernel(tc, q, k_dir, v, out):
             for line in range(LINES):
                 nc.sync.dma_start(out=dst[line * SIDE : (line + 1) * SIDE], in_=by_line[line])
 
-        q_raw = keep.tile([P, TILES, CHANNELS], BF16)
+        q_raw = {}
+        for columns in (False, True):
+            q_raw[columns] = keep.tile([P, TILES, CHANNELS], BF16, name="q_raw%d" % columns)
         k_raw = {}
         for direction in (LEFT, RIGHT, UP, DOWN):
             k_raw[direction] = keep.tile([P, TILES, CHANNELS], BF16, name="k_raw%d" % direction)
@@ -125,7 +135,7 @@ def tile_localdirectionalattention_pa_kernel(tc, q, k_dir, v, out):
         v_rows = keep.tile([P, TILES, CHANNELS], BF16)
 
         first_head, other_heads = [0], list(range(1, HEADS))
-        load_in_rows(q_raw, q[0], first_head)
+        load_in_rows(q_raw[False], q[0], first_head)
         load_in_rows(k_raw[UP], k_dir[UP, 0], first_head)
         load_in_rows(k_raw[DOWN], k_dir[DOWN, 0], first_head)
         nc.sync.dma_start(
@@ -133,9 +143,10 @@ def tile_localdirectionalattention_pa_kernel(tc, q, k_dir, v, out):
             in_=v[0].rearrange("(u p b) h d -> p u (b h d)", p=P, b=PAIR),
         )
         load_in_rows(v_rows, v[0], first_head + other_heads)
-        load_in_rows(q_raw, q[0], other_heads)
+        load_in_rows(q_raw[False], q[0], other_heads)
         load_in_rows(k_raw[UP], k_dir[UP, 0], other_heads)
         load_in_rows(k_raw[DOWN], k_dir[DOWN, 0], other_heads)
+        load_in_columns(q_raw[True], q[0])
         load_in_columns(k_raw[LEFT], k_dir[LEFT, 0])
         load_in_columns(k_raw[RIGHT], k_dir[RIGHT, 0])
         by_column = v[0].rearrange(
@@ -202,7 +213,7 @@ def tile_localdirectionalattention_pa_kernel(tc, q, k_dir, v, out):
         turned = {}
         q_t = {}
         k_t = {}
-        banks_of = {}
+        bank_of = {}
         staged_of = {}
         neg_max_of = {}
         row_sum = {}
@@ -215,59 +226,48 @@ def tile_localdirectionalattention_pa_kernel(tc, q, k_dir, v, out):
         inverse = {}
         side_sum = {}
 
-        def turn_inputs(g):
+        def turn_inputs(g, what):
             direction, h = groups[g]
-            sources = [("k_t", k_raw[direction])]
-            if direction == UP:
-                sources.append(("q_t", q_raw))
-            for name, raw in sources:
-                bank = psum_turn.tile([P, POSITIONS], BF16, tag="turn")
-                for i in range(TILES):
-                    nc.tensor.transpose(
-                        bank[:, i * P : (i + 1) * P],
-                        raw[:, i, h * WIDTH : (h + 1) * WIDTH],
-                        ident_bf16[:],
-                    )
-                turned[name] = bank
+            if what == "q" and not sees_smaller(direction):
+                return
+            raw = k_raw[direction] if what == "k" else q_raw[in_columns(direction)]
+            turned[what] = psum_turn.tile([P, POSITIONS], BF16, name="turned", tag="turn")
+            for i in range(TILES):
+                nc.tensor.transpose(
+                    turned[what][:, i * P : (i + 1) * P],
+                    raw[:, i, h * WIDTH : (h + 1) * WIDTH],
+                    ident_bf16[:],
+                )
 
-        def keep_inputs(g):
+        def keep_inputs(g, what):
             direction, h = groups[g]
-            k_t[g] = operands.tile([P, POSITIONS], BF16, name="k_t", tag="k_t")
-            nc.scalar.copy(out=k_t[g][:], in_=turned["k_t"][:])
-            if direction == UP:
-                q_t[(False, h)] = operands.tile([P, POSITIONS], BF16, name="q_t", tag="q_t")
+            if what == "k":
+                k_t[g] = operands.tile([P, POSITIONS], BF16, name="k_t", tag="k_t")
+                nc.scalar.copy(out=k_t[g][:], in_=turned["k"][:])
+            elif sees_smaller(direction):
+                q_t[h] = operands.tile([P, POSITIONS], BF16, name="q_t", tag="q_t")
                 if g == 0:
-                    nc.vector.tensor_copy(out=q_t[(False, h)][:], in_=turned["q_t"][:])
+                    nc.vector.tensor_copy(out=q_t[h][:], in_=turned["q"][:])
                 else:
-                    nc.scalar.copy(out=q_t[(False, h)][:], in_=turned["q_t"][:])
+                    nc.scalar.copy(out=q_t[h][:], in_=turned["q"][:])
 
-        def reorder_queries(h):
-            q_t[(True, h)] = keep.tile([P, POSITIONS], BF16, name="q_columns%d" % h)
+        def regroup_values(columns, b, h):
+            by_half = (
+                v_keys_columns[:].rearrange("p b u x -> p u b x") if columns else v_keys_rows[:]
+            )
+            head = slice(h * WIDTH, (h + 1) * WIDTH)
+            if h == 0:
+                v_grouped[b] = work.tile(
+                    [P, CHANNELS, HALVES, PAIR], BF16, name="v_grouped", tag="v_grouped", bufs=2, align_bytes=64
+                )
             nc.gpsimd.tensor_scalar(
-                out=q_t[(True, h)][:].rearrange("p (c r) -> p c r", r=SIDE),
-                in0=q_t[(False, h)][:].rearrange("p (r c) -> p c r", c=SIDE),
+                out=v_grouped[b][:, head],
+                in0=by_half[:, b * HALVES : (b + 1) * HALVES, :, head].rearrange("p u b x -> p x u b"),
                 scalar1=1.0,
                 scalar2=0.0,
                 op0=ALU.mult,
                 op1=ALU.add,
             )
-
-        def regroup_values(columns):
-            by_half = (
-                v_keys_columns[:].rearrange("p b u x -> p u b x") if columns else v_keys_rows[:]
-            )
-            for b in range(PASSES):
-                v_grouped[b] = work.tile(
-                    [P, CHANNELS, HALVES, PAIR], BF16, name="v_grouped", tag="v_grouped", bufs=2, align_bytes=64
-                )
-                nc.gpsimd.tensor_scalar(
-                    out=v_grouped[b][:],
-                    in0=by_half[:, b * HALVES : (b + 1) * HALVES].rearrange("p u b x -> p x u b"),
-                    scalar1=1.0,
-                    scalar2=0.0,
-                    op0=ALU.mult,
-                    op1=ALU.add,
-                )
 
         def quantise_values(columns):
             codes = keep.tile([P, PASSES * CHANNELS], U32, name="v_codes%d" % columns, align_bytes=64)
@@ -282,37 +282,35 @@ def tile_localdirectionalattention_pa_kernel(tc, q, k_dir, v, out):
             v_codes[columns] = codes
             v_scales[columns] = scales
 
-        def scores(g, i):
+        def scores(g, i, n):
             direction, h = groups[g]
             smaller = sees_smaller(direction)
             first, behind = seen_keys(direction, i)
             own_lo, own_hi = max(first, i * P), min(behind, (i + 1) * P)
-            banks = []
-            for b in pass_list(direction, i):
-                lo = max(first, b * K_PASS)
-                hi = min(behind, (b + 1) * K_PASS)
-                s_bank = psum_scores.tile([P, K_PASS], F32, tag="scores")
-                on_diagonal = lo <= own_lo < hi
+            b = pass_list(direction, i)[n]
+            lo = max(first, b * K_PASS)
+            hi = min(behind, (b + 1) * K_PASS)
+            s_bank = psum_scores.tile([P, K_PASS], F32, tag="scores")
+            on_diagonal = lo <= own_lo < hi
+            nc.tensor.matmul(
+                s_bank[:],
+                lhsT=q_t[h][:, i * P : (i + 1) * P],
+                rhs=k_t[g][:, b * K_PASS : (b + 1) * K_PASS],
+                start=True,
+                stop=not on_diagonal,
+            )
+            if on_diagonal:
                 nc.tensor.matmul(
-                    s_bank[:],
-                    lhsT=q_t[(in_columns(direction), h)][:, i * P : (i + 1) * P],
-                    rhs=k_t[g][:, b * K_PASS : (b + 1) * K_PASS],
-                    start=True,
-                    stop=not on_diagonal,
+                    s_bank[:, own_lo - b * K_PASS : own_hi - b * K_PASS],
+                    lhsT=ident_bf16[:],
+                    rhs=mask[smaller][:, own_lo - i * P : own_hi - i * P],
+                    start=False,
+                    stop=True,
                 )
-                if on_diagonal:
-                    nc.tensor.matmul(
-                        s_bank[:, own_lo - b * K_PASS : own_hi - b * K_PASS],
-                        lhsT=ident_bf16[:],
-                        rhs=mask[smaller][:, own_lo - i * P : own_hi - i * P],
-                        start=False,
-                        stop=True,
-                    )
-                banks.append((s_bank[:, lo - b * K_PASS : hi - b * K_PASS], lo, hi))
-            banks_of[(g, i)] = banks
+            bank_of[(g, i, n)] = (s_bank[:, lo - b * K_PASS : hi - b * K_PASS], lo, hi)
 
         def stage_scores(g, i, n):
-            in_psum, lo, hi = banks_of[(g, i)][n]
+            in_psum, lo, hi = bank_of[(g, i, n)]
             if n == 0:
                 staged_of[(g, i)] = work.tile([P, POSITIONS], F32, name="staged", tag="staged", bufs=6)
             lowest = work.tile([P, 1], F32, bufs=8)
@@ -331,7 +329,7 @@ def tile_localdirectionalattention_pa_kernel(tc, q, k_dir, v, out):
             direction, h = groups[g]
             first, behind = seen_keys(direction, i)
             e = e_home[(sees_smaller(direction), i)]
-            if i == TILE_ORDER[0]:
+            if i == tile_order(direction)[0]:
                 row_sum[g] = work.tile([P, TILES], F32, name="row_sum", tag="row_sum")
             nc.scalar.activation(
                 out=e[:, first:behind],
@@ -345,19 +343,19 @@ def tile_localdirectionalattention_pa_kernel(tc, q, k_dir, v, out):
                 own_lo, own_hi = max(first, i * P), min(behind, (i + 1) * P)
                 nc.gpsimd.memset(e[blind_rows(direction), own_lo:own_hi], 1.0)
 
-        def turn(g, i):
+        def turn(g, i, n):
             direction, h = groups[g]
             e_words = e_home[(sees_smaller(direction), i)][:].bitcast(F32)
-            e_t = psum_turn.tile([P, PASSES, HALVES, P], F32, tag="turn")
-            for n, b in enumerate(pass_list(direction, i)):
-                for u in range(HALVES):
-                    w0 = (b * HALVES + u) * P
-                    nc.tensor.transpose(e_t[:, n, u, :], e_words[:, w0 : w0 + P], ident_f32[:])
-            e_t_of[(g, i)] = e_t
+            if n == 0:
+                e_t_of[(g, i)] = psum_turn.tile([P, PASSES, HALVES, P], F32, name="e_t", tag="turn")
+            b = pass_list(direction, i)[n]
+            for u in range(HALVES):
+                w0 = (b * HALVES + u) * P
+                nc.tensor.transpose(e_t_of[(g, i)][:, n, u, :], e_words[:, w0 : w0 + P], ident_f32[:])
 
         def regroup(g, i):
             count = len(pass_list(groups[g][0], i))
-            grouped = work.tile([P, PASSES * K_PASS], BF16, align_bytes=64)
+            grouped = work.tile([P, PASSES * K_PASS], BF16, align_bytes=64, bufs=6)
             nc.scalar.copy(
                 out=grouped[:]
                 .bitcast(F32)[:, 0 : count * P * HALVES]
@@ -369,7 +367,7 @@ def tile_localdirectionalattention_pa_kernel(tc, q, k_dir, v, out):
         def quantise(g, i):
             direction, h = groups[g]
             passes = pass_list(direction, i)
-            if i == TILE_ORDER[0]:
+            if i == tile_order(direction)[0]:
                 e_codes[g] = operands.tile(
                     [P, TILES * PASSES * P], U32, name="e_codes", tag="e_codes", align_bytes=64
                 )
@@ -428,7 +426,7 @@ def tile_localdirectionalattention_pa_kernel(tc, q, k_dir, v, out):
             direction, h = groups[g]
             head = slice(h * WIDTH, (h + 1) * WIDTH)
             pv = pv_of[(g, tiles[0])]
-            if direction == UP and tiles[0] == TILE_ORDER[0]:
+            if direction == UP and tiles[0] == tile_order(direction)[0]:
                 side_sum[h] = work.tile([P, TILES, WIDTH], F32, name="side_sum", tag="side_sum", bufs=2)
             for n, i in enumerate(tiles):
                 acc = total[:, i, head] if in_columns(direction) else side_sum[h][:, i, :]
@@ -460,68 +458,75 @@ def tile_localdirectionalattention_pa_kernel(tc, q, k_dir, v, out):
                     out=total[line * SIDE : (line + 1) * SIDE, :, head], in_=out_columns[line][:, :, head]
                 )
 
-        def take_fifth(h):
-            head = slice(h * WIDTH, (h + 1) * WIDTH)
-            nc.gpsimd.tensor_scalar(
-                out=total[:, :, head], in0=total[:, :, head], scalar1=0.2, scalar2=0.0, op0=ALU.mult, op1=ALU.add
-            )
+        def take_fifth(h, first):
+            part = total[:, first : first + FIFTH_TILES, h * WIDTH : (h + 1) * WIDTH]
+            nc.gpsimd.tensor_scalar(out=part, in0=part, scalar1=0.2, scalar2=0.0, op0=ALU.mult, op1=ALU.add)
 
-        def unit(index):
-            g, position = divmod(index, TILES)
-            return g, TILE_ORDER[position]
+        slots = []
+        for g, (direction, h) in enumerate(groups):
+            for i in tile_order(direction):
+                count = len(pass_list(direction, i))
+                slots += [(g, i, n, n == count - 1) for n in range(count)]
 
-        n_units = len(groups) * TILES
-        turn_inputs(0)
-        keep_inputs(0)
+        def slot_at(index):
+            return slots[index] if 0 <= index < len(slots) else (None, None, None, False)
+
+        turn_inputs(0, "k")
+        turn_inputs(0, "q")
+        keep_inputs(0, "k")
+        keep_inputs(0, "q")
         for ahead in range(SCORE_LEAD):
-            scores(*unit(ahead))
-        for step in range(n_units + DRAIN):
-            g, position = divmod(step, TILES)
-            if step + SCORE_LEAD < n_units:
-                scores(*unit(step + SCORE_LEAD))
-            if step < n_units:
-                stage_scores(*unit(step), 0)
-            if TURN_LAG <= step < n_units + TURN_LAG:
-                turn(*unit(step - TURN_LAG))
-            if EXP_LAG <= step < n_units + EXP_LAG:
-                exponential(*unit(step - EXP_LAG))
-            if TURN_LAG <= step < n_units + TURN_LAG:
-                regroup(*unit(step - TURN_LAG))
-            if QUANT_LAG <= step < n_units + QUANT_LAG:
-                quantise(*unit(step - QUANT_LAG))
-            if step < n_units and len(banks_of[unit(step)]) == PASSES:
-                stage_scores(*unit(step), 1)
+            scores(*slots[ahead][:3])
+        for slot in range(len(slots) + DRAIN):
+            g, position = divmod(slot, GROUP_SLOTS)
+            if slot + SCORE_LEAD < len(slots):
+                scores(*slots[slot + SCORE_LEAD][:3])
+            if slot < len(slots):
+                stage_scores(*slots[slot][:3])
+            turning, turning_tile, turning_pass, turned_all = slot_at(slot - TURN_LAG)
+            if turning is not None:
+                turn(turning, turning_tile, turning_pass)
+            staged, staged_tile, staged_bank, staged_all = slot_at(slot - EXP_LAG)
+            if staged_all:
+                exponential(staged, staged_tile)
+            if turned_all:
+                regroup(turning, turning_tile)
+            grouped, grouped_tile, grouped_pass, grouped_all = slot_at(slot - QUANT_LAG)
+            if grouped_all:
+                quantise(grouped, grouped_tile)
 
             if g + 1 < len(groups):
-                if position == AT_TURN_INPUTS:
-                    turn_inputs(g + 1)
-                if position == AT_KEEP_INPUTS:
-                    keep_inputs(g + 1)
-            if g < len(groups) and groups[g][0] == UP and position == AT_REORDER_QUERIES:
-                reorder_queries(groups[g][1])
-            if g < len(groups) and groups[g] in ((LEFT, 0), (UP, 0)):
-                if position == AT_REGROUP_VALUES:
-                    regroup_values(in_columns(groups[g][0]))
-                if position == AT_QUANTISE_VALUES:
-                    quantise_values(in_columns(groups[g][0]))
-            for ended in range(max(0, g - 3), min(g, len(groups))):
-                since = step - (ended + 1) * TILES
+                if position == AT_TURN_KEYS:
+                    turn_inputs(g + 1, "k")
+                if position == AT_KEEP_KEYS:
+                    keep_inputs(g + 1, "k")
+                if position == AT_TURN_QUERIES:
+                    turn_inputs(g + 1, "q")
+                if position == AT_KEEP_QUERIES:
+                    keep_inputs(g + 1, "q")
+            if g in (0, len(groups) // 2 - 1) and position < PASSES * HEADS:
+                regroup_values(g > 0, position // HEADS, position % HEADS)
+            if g in (0, len(groups) // 2) and position == AT_QUANTISE_VALUES:
+                quantise_values(g > 0)
+            for ended in range(max(0, g - 4), min(g, len(groups))):
+                since = slot - (ended + 1) * GROUP_SLOTS
                 direction, h = groups[ended]
+                tiles = tile_order(direction)
                 if since == AT_PREPARE_SUMS:
                     prepare_sums(ended)
-                if since == AT_FIRST_ROUND:
-                    weighted_values(ended, TILE_ORDER[:ROUND])
                 if since == AT_NORMALISE:
                     normalise(ended)
+                if since == AT_FIRST_ROUND:
+                    weighted_values(ended, tiles[:ROUND])
                 if since == AT_FIRST_SUM:
-                    sum_up(ended, TILE_ORDER[:ROUND])
+                    sum_up(ended, tiles[:ROUND])
                 if since == AT_SECOND_ROUND:
-                    weighted_values(ended, TILE_ORDER[ROUND:])
+                    weighted_values(ended, tiles[ROUND:])
                 if since == AT_SECOND_SUM:
-                    sum_up(ended, TILE_ORDER[ROUND:])
+                    sum_up(ended, tiles[ROUND:])
                 if direction == DOWN and since == AT_PARK:
                     park(h)
                 if direction == DOWN and since == AT_FETCH:
                     fetch(h)
-                if direction == DOWN and since == AT_FIFTH:
-                    take_fifth(h)
+                if direction == DOWN and AT_FIFTH <= since < AT_FIFTH + TILES // FIFTH_TILES:
+                    take_fifth(h, (since - AT_FIFTH) * FIFTH_TILES)

@@ -26,6 +26,8 @@ CHUNKS = K_PASS // P
 PAIR = 2
 HALVES = PACK // PAIR
 NEG = -1.0e9
+ALL_TILES = slice(0, TILES)
+HALF_TILES = [slice(0, TILES // 2), slice(TILES // 2, TILES)]
 
 LEFT, RIGHT, UP, DOWN = 0, 1, 2, 3
 FLOPS = 2 * 2 * 4 * HEADS * POSITIONS * POSITIONS * WIDTH
@@ -43,7 +45,7 @@ AT_TURN_QUERIES = 4
 AT_KEEP_QUERIES = 6
 AT_QUANTISE_VALUES = 10
 AT_PREPARE_SUMS = 4
-AT_NORMALISE = 6
+AT_NORMALISE = 8
 AT_FIRST_ROUND = 7
 AT_FIRST_SUM = 10
 AT_SECOND_ROUND = 13
@@ -104,6 +106,20 @@ def tile_localdirectionalattention_pa_kernel(tc, q, k_dir, v, out):
     groups = [(d, h) for h in range(HEADS) for d in (UP, DOWN)]
     groups += [(d, h) for h in range(HEADS) for d in (LEFT, RIGHT)]
 
+    orders = [tile_order(direction) for direction, h in groups]
+    orders[-1] = [0, 4, 1, 5, 2, 3, 6, 7]
+
+    def rounds_of(g):
+        tiles = orders[g]
+        rounds = [(tiles[:ROUND], AT_FIRST_ROUND, AT_FIRST_SUM)]
+        if g < len(groups) - 1:
+            return rounds + [(tiles[ROUND:], AT_SECOND_ROUND, AT_SECOND_SUM)]
+        half = ROUND // 2
+        return rounds + [
+            (tiles[ROUND:-half], AT_SECOND_ROUND - 2, AT_SECOND_ROUND - 1),
+            (tiles[-half:], AT_SECOND_ROUND, AT_SECOND_ROUND + 1),
+        ]
+
     with ExitStack() as ctx:
         keep = ctx.enter_context(tc.tile_pool(name="keep", bufs=1))
         operands = ctx.enter_context(tc.tile_pool(name="operands", bufs=2))
@@ -113,10 +129,10 @@ def tile_localdirectionalattention_pa_kernel(tc, q, k_dir, v, out):
         psum_pv = ctx.enter_context(tc.psum_pool(name="psum_pv", bufs=1))
         ctx.enter_context(tc.manual_schedule())
 
-        def load_in_rows(dst, src, heads):
+        def load_in_rows(dst, src, heads, tiles=ALL_TILES):
             cols = slice(heads[0] * WIDTH, (heads[-1] + 1) * WIDTH)
             nc.sync.dma_start(
-                out=dst[:, :, cols], in_=src.rearrange("(i p) h d -> p i (h d)", p=P)[:, :, cols]
+                out=dst[:, tiles, cols], in_=src.rearrange("(i p) h d -> p i (h d)", p=P)[:, tiles, cols]
             )
 
         def load_in_columns(dst, src):
@@ -135,8 +151,9 @@ def tile_localdirectionalattention_pa_kernel(tc, q, k_dir, v, out):
         v_rows = keep.tile([P, TILES, CHANNELS], BF16)
 
         first_head, other_heads = [0], list(range(1, HEADS))
-        load_in_rows(q_raw[False], q[0], first_head)
-        load_in_rows(k_raw[UP], k_dir[UP, 0], first_head)
+        for half in HALF_TILES:
+            load_in_rows(q_raw[False], q[0], first_head, half)
+            load_in_rows(k_raw[UP], k_dir[UP, 0], first_head, half)
         load_in_rows(k_raw[DOWN], k_dir[DOWN, 0], first_head)
         nc.sync.dma_start(
             out=v_keys_rows[:].rearrange("p u b x -> p u (b x)"),
@@ -226,30 +243,34 @@ def tile_localdirectionalattention_pa_kernel(tc, q, k_dir, v, out):
         inverse = {}
         side_sum = {}
 
-        def turn_inputs(g, what):
+        def turn_inputs(g, what, tiles=ALL_TILES):
             direction, h = groups[g]
             if what == "q" and not sees_smaller(direction):
                 return
             raw = k_raw[direction] if what == "k" else q_raw[in_columns(direction)]
-            turned[what] = psum_turn.tile([P, POSITIONS], BF16, name="turned", tag="turn")
-            for i in range(TILES):
+            bank = psum_turn.tile([P, (tiles.stop - tiles.start) * P], BF16, tag="turn")
+            for n in range(tiles.stop - tiles.start):
                 nc.tensor.transpose(
-                    turned[what][:, i * P : (i + 1) * P],
-                    raw[:, i, h * WIDTH : (h + 1) * WIDTH],
+                    bank[:, n * P : (n + 1) * P],
+                    raw[:, tiles.start + n, h * WIDTH : (h + 1) * WIDTH],
                     ident_bf16[:],
                 )
+            turned[(what, tiles.start)] = bank
 
-        def keep_inputs(g, what):
+        def keep_inputs(g, what, tiles=ALL_TILES):
             direction, h = groups[g]
-            if what == "k":
+            if what == "q" and not sees_smaller(direction):
+                return
+            if tiles.start == 0 and what == "k":
                 k_t[g] = operands.tile([P, POSITIONS], BF16, name="k_t", tag="k_t")
-                nc.scalar.copy(out=k_t[g][:], in_=turned["k"][:])
-            elif sees_smaller(direction):
+            if tiles.start == 0 and what == "q":
                 q_t[h] = operands.tile([P, POSITIONS], BF16, name="q_t", tag="q_t")
-                if g == 0:
-                    nc.vector.tensor_copy(out=q_t[h][:], in_=turned["q"][:])
-                else:
-                    nc.scalar.copy(out=q_t[h][:], in_=turned["q"][:])
+            kept = k_t[g] if what == "k" else q_t[h]
+            part = kept[:, tiles.start * P : tiles.stop * P]
+            if g == 0 and what == "q":
+                nc.vector.tensor_copy(out=part, in_=turned[(what, tiles.start)][:])
+            else:
+                nc.scalar.copy(out=part, in_=turned[(what, tiles.start)][:])
 
         def regroup_values(columns, b, h):
             by_half = (
@@ -329,7 +350,7 @@ def tile_localdirectionalattention_pa_kernel(tc, q, k_dir, v, out):
             direction, h = groups[g]
             first, behind = seen_keys(direction, i)
             e = e_home[(sees_smaller(direction), i)]
-            if i == tile_order(direction)[0]:
+            if i == orders[g][0]:
                 row_sum[g] = work.tile([P, TILES], F32, name="row_sum", tag="row_sum")
             nc.scalar.activation(
                 out=e[:, first:behind],
@@ -367,7 +388,7 @@ def tile_localdirectionalattention_pa_kernel(tc, q, k_dir, v, out):
         def quantise(g, i):
             direction, h = groups[g]
             passes = pass_list(direction, i)
-            if i == tile_order(direction)[0]:
+            if i == orders[g][0]:
                 e_codes[g] = operands.tile(
                     [P, TILES * PASSES * P], U32, name="e_codes", tag="e_codes", align_bytes=64
                 )
@@ -396,11 +417,14 @@ def tile_localdirectionalattention_pa_kernel(tc, q, k_dir, v, out):
             inverse[g] = work.tile([P, TILES], F32, name="inverse", tag="inverse")
             nc.vector.reciprocal(out=inverse[g][:], in_=divisor[g][:])
 
-        def weighted_values(g, tiles):
+        def weighted_values(g, tiles, last):
             direction, h = groups[g]
             smaller = sees_smaller(direction)
             columns = in_columns(direction)
-            pv = psum_pv.tile([P, ROUND, WIDTH], F32, tag="pv")
+            if last:
+                pv = psum_scores.tile([P, ROUND, WIDTH], F32, name="pv_last", tag="scores")
+            else:
+                pv = psum_pv.tile([P, ROUND, WIDTH], F32, name="pv", tag="pv")
             for n, i in enumerate(tiles):
                 passes = pass_list(direction, i)
                 lhs = []
@@ -422,11 +446,11 @@ def tile_localdirectionalattention_pa_kernel(tc, q, k_dir, v, out):
                     )
             pv_of[(g, tiles[0])] = pv
 
-        def sum_up(g, tiles):
+        def sum_up(g, tiles, last):
             direction, h = groups[g]
             head = slice(h * WIDTH, (h + 1) * WIDTH)
             pv = pv_of[(g, tiles[0])]
-            if direction == UP and tiles[0] == tile_order(direction)[0]:
+            if direction == UP and tiles[0] == orders[g][0]:
                 side_sum[h] = work.tile([P, TILES, WIDTH], F32, name="side_sum", tag="side_sum", bufs=2)
             for n, i in enumerate(tiles):
                 acc = total[:, i, head] if in_columns(direction) else side_sum[h][:, i, :]
@@ -442,7 +466,8 @@ def tile_localdirectionalattention_pa_kernel(tc, q, k_dir, v, out):
             if direction == RIGHT:
                 for first, behind in runs(tiles):
                     for line in range(LINES):
-                        nc.sync.dma_start(
+                        queue = nc.scalar if last and line >= LINES // 2 else nc.sync
+                        queue.dma_start(
                             out=out_columns[line][:, first:behind, head],
                             in_=total[line * SIDE : (line + 1) * SIDE, first:behind, head],
                         )
@@ -464,17 +489,18 @@ def tile_localdirectionalattention_pa_kernel(tc, q, k_dir, v, out):
 
         slots = []
         for g, (direction, h) in enumerate(groups):
-            for i in tile_order(direction):
+            for i in orders[g]:
                 count = len(pass_list(direction, i))
                 slots += [(g, i, n, n == count - 1) for n in range(count)]
 
         def slot_at(index):
             return slots[index] if 0 <= index < len(slots) else (None, None, None, False)
 
-        turn_inputs(0, "k")
-        turn_inputs(0, "q")
-        keep_inputs(0, "k")
-        keep_inputs(0, "q")
+        for half in HALF_TILES:
+            for what in ("q", "k"):
+                turn_inputs(0, what, half)
+            for what in ("q", "k"):
+                keep_inputs(0, what, half)
         for ahead in range(SCORE_LEAD):
             scores(*slots[ahead][:3])
         for slot in range(len(slots) + DRAIN):
@@ -504,26 +530,27 @@ def tile_localdirectionalattention_pa_kernel(tc, q, k_dir, v, out):
                     turn_inputs(g + 1, "q")
                 if position == AT_KEEP_QUERIES:
                     keep_inputs(g + 1, "q")
-            if g in (0, len(groups) // 2 - 1) and position < PASSES * HEADS:
-                regroup_values(g > 0, position // HEADS, position % HEADS)
+            if g == 0 and position < PASSES * HEADS:
+                regroup_values(False, position // HEADS, position % HEADS)
+            pass_of_v = g - (len(groups) // 2 - PASSES)
+            if 0 <= pass_of_v < PASSES and position % (GROUP_SLOTS // HEADS) == 0:
+                regroup_values(True, pass_of_v, position // (GROUP_SLOTS // HEADS))
             if g in (0, len(groups) // 2) and position == AT_QUANTISE_VALUES:
                 quantise_values(g > 0)
             for ended in range(max(0, g - 4), min(g, len(groups))):
                 since = slot - (ended + 1) * GROUP_SLOTS
                 direction, h = groups[ended]
-                tiles = tile_order(direction)
+                rounds = rounds_of(ended)
                 if since == AT_PREPARE_SUMS:
                     prepare_sums(ended)
                 if since == AT_NORMALISE:
                     normalise(ended)
-                if since == AT_FIRST_ROUND:
-                    weighted_values(ended, tiles[:ROUND])
-                if since == AT_FIRST_SUM:
-                    sum_up(ended, tiles[:ROUND])
-                if since == AT_SECOND_ROUND:
-                    weighted_values(ended, tiles[ROUND:])
-                if since == AT_SECOND_SUM:
-                    sum_up(ended, tiles[ROUND:])
+                for tiles, at_products, at_sums in rounds:
+                    last = ended == len(groups) - 1 and tiles[-1] == orders[ended][-1]
+                    if since == at_products:
+                        weighted_values(ended, tiles, last)
+                    if since == at_sums:
+                        sum_up(ended, tiles, last)
                 if direction == DOWN and since == AT_PARK:
                     park(h)
                 if direction == DOWN and since == AT_FETCH:

@@ -43,7 +43,7 @@ AT_TURN_KEYS = 1
 AT_KEEP_KEYS = 3
 AT_TURN_QUERIES = 4
 AT_KEEP_QUERIES = 6
-AT_QUANTISE_VALUES = 10
+AT_QUANTISE_VALUES = 3
 AT_PREPARE_SUMS = 4
 AT_NORMALISE = 8
 AT_FIRST_ROUND = 7
@@ -350,7 +350,7 @@ def tile_localdirectionalattention_pa_kernel(tc, q, k_dir, v, out):
             direction, h = groups[g]
             first, behind = seen_keys(direction, i)
             e = e_home[(sees_smaller(direction), i)]
-            if i == orders[g][0]:
+            if g not in row_sum:
                 row_sum[g] = work.tile([P, TILES], F32, name="row_sum", tag="row_sum")
             nc.scalar.activation(
                 out=e[:, first:behind],
@@ -364,43 +364,77 @@ def tile_localdirectionalattention_pa_kernel(tc, q, k_dir, v, out):
                 own_lo, own_hi = max(first, i * P), min(behind, (i + 1) * P)
                 nc.gpsimd.memset(e[blind_rows(direction), own_lo:own_hi], 1.0)
 
+        def bank_list(g, quad):
+            direction, h = groups[g]
+            tiles = orders[g][quad * ROUND : (quad + 1) * ROUND]
+            wide = [[(i, 0), (i, 1)] for i in tiles if len(pass_list(direction, i)) == PASSES]
+            shared = [(i, 0) for i in tiles if len(pass_list(direction, i)) == 1]
+            if g == len(groups) - 1:
+                return wide + [shared]
+            return [wide[0], shared, wide[1]]
+
+        def quantise_list(g):
+            return [[0, 1], [2]] if g == len(groups) - 1 else [[0], [1, 2]]
+
         def turn(g, i, n):
             direction, h = groups[g]
+            quad = orders[g].index(i) // ROUND
             e_words = e_home[(sees_smaller(direction), i)][:].bitcast(F32)
-            if n == 0:
-                e_t_of[(g, i)] = psum_turn.tile([P, PASSES, HALVES, P], F32, name="e_t", tag="turn")
             b = pass_list(direction, i)[n]
-            for u in range(HALVES):
-                w0 = (b * HALVES + u) * P
-                nc.tensor.transpose(e_t_of[(g, i)][:, n, u, :], e_words[:, w0 : w0 + P], ident_f32[:])
+            for bank, passes in enumerate(bank_list(g, quad)):
+                if (i, n) in passes:
+                    if (g, quad, bank) not in e_t_of:
+                        e_t_of[(g, quad, bank)] = psum_turn.tile(
+                            [P, PASSES, HALVES, P], F32, name="e_t", tag="turn"
+                        )
+                    for u in range(HALVES):
+                        w0 = (b * HALVES + u) * P
+                        nc.tensor.transpose(
+                            e_t_of[(g, quad, bank)][:, passes.index((i, n)), u, :],
+                            e_words[:, w0 : w0 + P],
+                            ident_f32[:],
+                        )
 
-        def regroup(g, i):
-            count = len(pass_list(groups[g][0], i))
-            grouped = work.tile([P, PASSES * K_PASS], BF16, align_bytes=64, bufs=6)
-            nc.scalar.copy(
-                out=grouped[:]
-                .bitcast(F32)[:, 0 : count * P * HALVES]
-                .rearrange("p (n w u) -> p n w u", n=count, u=HALVES),
-                in_=e_t_of[(g, i)][:, 0:count].rearrange("p n u w -> p n w u"),
-            )
-            grouped_of[(g, i)] = grouped
+        def regroup(g, quad, bank):
+            for banks in quantise_list(g):
+                if bank not in banks:
+                    continue
+                key = (g, quad, banks[0])
+                if key not in grouped_of:
+                    grouped_of[key] = work.tile(
+                        [P, len(banks), PASSES * K_PASS],
+                        BF16,
+                        name="grouped",
+                        tag="grouped%d" % len(banks),
+                        align_bytes=64,
+                    )
+                nc.scalar.copy(
+                    out=grouped_of[key][:, banks.index(bank)]
+                    .bitcast(F32)
+                    .rearrange("p (n w u) -> p n w u", n=PASSES, u=HALVES),
+                    in_=e_t_of[(g, quad, bank)][:].rearrange("p n u w -> p n w u"),
+                )
 
-        def quantise(g, i):
-            direction, h = groups[g]
-            passes = pass_list(direction, i)
-            if i == orders[g][0]:
+        def quantise(g, quad, banks):
+            if g not in e_codes:
                 e_codes[g] = operands.tile(
-                    [P, TILES * PASSES * P], U32, name="e_codes", tag="e_codes", align_bytes=64
+                    [P, GROUP_SLOTS * P], U32, name="e_codes", tag="e_codes", align_bytes=64
                 )
                 e_scales[g] = operands.tile(
-                    [P, TILES * PASSES * P], U8, name="e_scales", tag="e_scales", align_bytes=64
+                    [P, GROUP_SLOTS * P], U8, name="e_scales", tag="e_scales", align_bytes=64
                 )
-            words = slice((i * PASSES + passes[0]) * P, (i * PASSES + passes[-1] + 1) * P)
+            lo = quad * GROUP_SLOTS // 2 + banks[0] * PASSES
+            words = slice(lo * P, (lo + len(banks) * PASSES) * P)
             nc.vector.quantize_mx(
                 out=e_codes[g][:, words].bitcast(FP8X4),
                 scales=e_scales[g][:, words],
-                in_=grouped_of[(g, i)][:, 0 : len(passes) * K_PASS],
+                in_=grouped_of[(g, quad, banks[0])][:].rearrange("p n k -> p (n k)"),
             )
+
+        def place(g, i, n):
+            quad = orders[g].index(i) // ROUND
+            in_order = [which for passes in bank_list(g, quad) for which in passes]
+            return quad * GROUP_SLOTS // 2 + in_order.index((i, n))
 
         def prepare_sums(g):
             direction, h = groups[g]
@@ -428,8 +462,9 @@ def tile_localdirectionalattention_pa_kernel(tc, q, k_dir, v, out):
             for n, i in enumerate(tiles):
                 passes = pass_list(direction, i)
                 lhs = []
-                for b in passes:
-                    words = slice((i * PASSES + b) * P, (i * PASSES + b + 1) * P)
+                for m, b in enumerate(passes):
+                    at = place(g, i, m)
+                    words = slice(at * P, (at + 1) * P)
                     lhs.append((b, e_codes[g][:, words], e_scales[g][:, words]))
                 if i == blind_tile(direction):
                     lhs.append((PASSES - 1 - passes[0], blind_codes[smaller][:], blind_scales[smaller][:]))
@@ -446,7 +481,7 @@ def tile_localdirectionalattention_pa_kernel(tc, q, k_dir, v, out):
                     )
             pv_of[(g, tiles[0])] = pv
 
-        def sum_up(g, tiles, last):
+        def sum_up(g, tiles):
             direction, h = groups[g]
             head = slice(h * WIDTH, (h + 1) * WIDTH)
             pv = pv_of[(g, tiles[0])]
@@ -466,8 +501,7 @@ def tile_localdirectionalattention_pa_kernel(tc, q, k_dir, v, out):
             if direction == RIGHT:
                 for first, behind in runs(tiles):
                     for line in range(LINES):
-                        queue = nc.scalar if last and line >= LINES // 2 else nc.sync
-                        queue.dma_start(
+                        nc.sync.dma_start(
                             out=out_columns[line][:, first:behind, head],
                             in_=total[line * SIDE : (line + 1) * SIDE, first:behind, head],
                         )
@@ -488,13 +522,23 @@ def tile_localdirectionalattention_pa_kernel(tc, q, k_dir, v, out):
             nc.gpsimd.tensor_scalar(out=part, in0=part, scalar1=0.2, scalar2=0.0, op0=ALU.mult, op1=ALU.add)
 
         slots = []
+        exponentials, regroups, quantises = {}, {}, {}
         for g, (direction, h) in enumerate(groups):
+            for pair in range(TILES // 2):
+                tiles = sorted(orders[g][2 * pair : 2 * pair + 2], key=lambda i: -len(pass_list(direction, i)))
+                for n in range(PASSES):
+                    slots += [(g, i, n) for i in tiles if n < len(pass_list(direction, i))]
             for i in orders[g]:
-                count = len(pass_list(direction, i))
-                slots += [(g, i, n, n == count - 1) for n in range(count)]
-
-        def slot_at(index):
-            return slots[index] if 0 <= index < len(slots) else (None, None, None, False)
+                last = slots.index((g, i, len(pass_list(direction, i)) - 1))
+                exponentials.setdefault(last + EXP_LAG, []).append((g, i))
+            for quad in range(TILES // ROUND):
+                ready = []
+                for passes in bank_list(g, quad):
+                    ready.append(max(slots.index((g, i, n)) for i, n in passes))
+                    regroups.setdefault(ready[-1] + TURN_LAG, []).append((g, quad, len(ready) - 1))
+                for banks in quantise_list(g):
+                    last = max(ready[n] for n in banks)
+                    quantises.setdefault(last + QUANT_LAG, []).append((g, quad, banks))
 
         for half in HALF_TILES:
             for what in ("q", "k"):
@@ -502,24 +546,21 @@ def tile_localdirectionalattention_pa_kernel(tc, q, k_dir, v, out):
             for what in ("q", "k"):
                 keep_inputs(0, what, half)
         for ahead in range(SCORE_LEAD):
-            scores(*slots[ahead][:3])
+            scores(*slots[ahead])
         for slot in range(len(slots) + DRAIN):
             g, position = divmod(slot, GROUP_SLOTS)
             if slot + SCORE_LEAD < len(slots):
-                scores(*slots[slot + SCORE_LEAD][:3])
+                scores(*slots[slot + SCORE_LEAD])
             if slot < len(slots):
-                stage_scores(*slots[slot][:3])
-            turning, turning_tile, turning_pass, turned_all = slot_at(slot - TURN_LAG)
-            if turning is not None:
-                turn(turning, turning_tile, turning_pass)
-            staged, staged_tile, staged_bank, staged_all = slot_at(slot - EXP_LAG)
-            if staged_all:
-                exponential(staged, staged_tile)
-            if turned_all:
-                regroup(turning, turning_tile)
-            grouped, grouped_tile, grouped_pass, grouped_all = slot_at(slot - QUANT_LAG)
-            if grouped_all:
-                quantise(grouped, grouped_tile)
+                stage_scores(*slots[slot])
+            if 0 <= slot - TURN_LAG < len(slots):
+                turn(*slots[slot - TURN_LAG])
+            for which in exponentials.get(slot, []):
+                exponential(*which)
+            for which in regroups.get(slot, []):
+                regroup(*which)
+            for which in quantises.get(slot, []):
+                quantise(*which)
 
             if g + 1 < len(groups):
                 if position == AT_TURN_KEYS:
@@ -535,8 +576,8 @@ def tile_localdirectionalattention_pa_kernel(tc, q, k_dir, v, out):
             pass_of_v = g - (len(groups) // 2 - PASSES)
             if 0 <= pass_of_v < PASSES and position % (GROUP_SLOTS // HEADS) == 0:
                 regroup_values(True, pass_of_v, position // (GROUP_SLOTS // HEADS))
-            if g in (0, len(groups) // 2) and position == AT_QUANTISE_VALUES:
-                quantise_values(g > 0)
+            if g in (1, len(groups) // 2) and position == AT_QUANTISE_VALUES:
+                quantise_values(g > 1)
             for ended in range(max(0, g - 4), min(g, len(groups))):
                 since = slot - (ended + 1) * GROUP_SLOTS
                 direction, h = groups[ended]
@@ -550,7 +591,7 @@ def tile_localdirectionalattention_pa_kernel(tc, q, k_dir, v, out):
                     if since == at_products:
                         weighted_values(ended, tiles, last)
                     if since == at_sums:
-                        sum_up(ended, tiles, last)
+                        sum_up(ended, tiles)
                 if direction == DOWN and since == AT_PARK:
                     park(h)
                 if direction == DOWN and since == AT_FETCH:

from contextlib import ExitStack

import concourse.mybir as mybir
from concourse.masks import make_identity

F32 = mybir.dt.float32
BF16 = mybir.dt.bfloat16
U32 = mybir.dt.uint32
U8 = mybir.dt.uint8
FP8X4 = mybir.dt.float8_e4m3fn_x4
ALU = mybir.AluOpType
ACT = mybir.ActivationFunctionType

P = 128
SIDE = 32
POSITIONS = SIDE * SIDE
HEADS = 4
WIDTH = 128
CHANNELS = HEADS * WIDTH
TILES = POSITIONS // P
LINES = P // SIDE
PACK = 4
K_PASS = P * PACK
PASSES = POSITIONS // K_PASS
CHUNKS = K_PASS // P
PAIR = 2
HALVES = PACK // PAIR
NEG = -1.0e9
ALL_TILES = slice(0, TILES)
HALF_TILES = [slice(0, TILES // 2), slice(TILES // 2, TILES)]

LEFT, RIGHT, UP, DOWN = 0, 1, 2, 3
FLOPS = 2 * 2 * 4 * HEADS * POSITIONS * POSITIONS * WIDTH

ROUND = CHUNKS

SCORE_LEAD = 2
EXP_LAG = 3
TURN_LAG = 8
QUANT_LAG = 13
GROUP_SLOTS = TILES // 2 * (1 + PASSES)
AT_TURN_KEYS = 1
AT_KEEP_KEYS = 3
AT_TURN_QUERIES = 4
AT_KEEP_QUERIES = 6
AT_QUANTISE_VALUES = 3
AT_PREPARE_SUMS = 4
AT_NORMALISE = 8
AT_FIRST_ROUND = 7
AT_FIRST_SUM = 10
AT_SECOND_ROUND = 13
AT_SECOND_SUM = 16
AT_PARK = 17
AT_FETCH = 29
AT_FIFTH = 35
FIFTH_TILES = 2
DRAIN = AT_SECOND_SUM + 1


def tile_order(direction):
    order = []
    for a in range(TILES // 2):
        order += [a, TILES - 1 - a] if sees_smaller(direction) else [TILES - 1 - a, a]
    return order


def sees_smaller(direction):
    return direction in (LEFT, UP)


def in_columns(direction):
    return direction in (LEFT, RIGHT)


def seen_keys(direction, i):
    if sees_smaller(direction):
        return 0, (i + 1) * P - SIDE
    return i * P + SIDE, POSITIONS


def pass_list(direction, i):
    lo, hi = seen_keys(direction, i)
    return list(range(lo // K_PASS, (hi - 1) // K_PASS + 1))


def blind_tile(direction):
    return 0 if sees_smaller(direction) else TILES - 1


def blind_rows(direction):
    return slice(0, SIDE) if sees_smaller(direction) else slice(P - SIDE, P)


def runs(tiles):
    spans = []
    for i in sorted(tiles):
        if spans and spans[-1][1] == i:
            spans[-1] = (spans[-1][0], i + 1)
        else:
            spans.append((i, i + 1))
    return spans


def tile_localdirectionalattention_pa_kernel(tc, q, k_dir, v, out):
    nc = tc.nc
    groups = [(d, h) for h in range(HEADS) for d in (UP, DOWN)]
    groups += [(d, h) for h in range(HEADS) for d in (LEFT, RIGHT)]

    orders = [tile_order(direction) for direction, h in groups]
    orders[-1] = [0, 4, 1, 5, 2, 3, 6, 7]

    def rounds_of(g):
        tiles = orders[g]
        rounds = [(tiles[:ROUND], AT_FIRST_ROUND, AT_FIRST_SUM)]
        if g < len(groups) - 1:
            return rounds + [(tiles[ROUND:], AT_SECOND_ROUND, AT_SECOND_SUM)]
        half = ROUND // 2
        return rounds + [
            (tiles[ROUND:-half], AT_SECOND_ROUND - 2, AT_SECOND_ROUND - 1),
            (tiles[-half:], AT_SECOND_ROUND, AT_SECOND_ROUND + 1),
        ]

    with ExitStack() as ctx:
        keep = ctx.enter_context(tc.tile_pool(name="keep", bufs=1))
        operands = ctx.enter_context(tc.tile_pool(name="operands", bufs=2))
        work = ctx.enter_context(tc.tile_pool(name="work", bufs=4))
        psum_scores = ctx.enter_context(tc.psum_pool(name="psum_scores", bufs=3))
        psum_turn = ctx.enter_context(tc.psum_pool(name="psum_turn", bufs=4))
        psum_pv = ctx.enter_context(tc.psum_pool(name="psum_pv", bufs=1))
        ctx.enter_context(tc.manual_schedule())

        def load_in_rows(dst, src, heads, tiles=ALL_TILES):
            cols = slice(heads[0] * WIDTH, (heads[-1] + 1) * WIDTH)
            nc.sync.dma_start(
                out=dst[:, tiles, cols], in_=src.rearrange("(i p) h d -> p i (h d)", p=P)[:, tiles, cols]
            )

        def load_in_columns(dst, src):
            by_line = src.rearrange("(r i l) h d -> l r i (h d)", r=SIDE, i=TILES, l=LINES)
            for line in range(LINES):
                nc.sync.dma_start(out=dst[line * SIDE : (line + 1) * SIDE], in_=by_line[line])

        q_raw = {}
        for columns in (False, True):
            q_raw[columns] = keep.tile([P, TILES, CHANNELS], BF16, name="q_raw%d" % columns)
        k_raw = {}
        for direction in (LEFT, RIGHT, UP, DOWN):
            k_raw[direction] = keep.tile([P, TILES, CHANNELS], BF16, name="k_raw%d" % direction)
        v_keys_rows = keep.tile([P, PASSES * HALVES, PAIR, CHANNELS], BF16)
        v_keys_columns = keep.tile([P, PAIR, PASSES * HALVES, CHANNELS], BF16)
        v_rows = keep.tile([P, TILES, CHANNELS], BF16)

        first_head, other_heads = [0], list(range(1, HEADS))
        for half in HALF_TILES:
            load_in_rows(q_raw[False], q[0], first_head, half)
            load_in_rows(k_raw[UP], k_dir[UP, 0], first_head, half)
        load_in_rows(k_raw[DOWN], k_dir[DOWN, 0], first_head)
        nc.sync.dma_start(
            out=v_keys_rows[:].rearrange("p u b x -> p u (b x)"),
            in_=v[0].rearrange("(u p b) h d -> p u (b h d)", p=P, b=PAIR),
        )
        load_in_rows(v_rows, v[0], first_head + other_heads)
        load_in_rows(q_raw[False], q[0], other_heads)
        load_in_rows(k_raw[UP], k_dir[UP, 0], other_heads)
        load_in_rows(k_raw[DOWN], k_dir[DOWN, 0], other_heads)
        load_in_columns(q_raw[True], q[0])
        load_in_columns(k_raw[LEFT], k_dir[LEFT, 0])
        load_in_columns(k_raw[RIGHT], k_dir[RIGHT, 0])
        by_column = v[0].rearrange(
            "(r b u c) h d -> c r (b u) (h d)", r=SIDE // PAIR, b=PAIR, u=PASSES * HALVES, c=8
        )
        for c in range(8):
            nc.sync.dma_start(
                out=v_keys_columns[c * 16 : (c + 1) * 16].rearrange("p b u x -> p (b u) x"),
                in_=by_column[c],
            )

        ident_bf16 = keep.tile([P, P], BF16)
        make_identity(nc, ident_bf16[:])
        ident_f32 = keep.tile([P, P], F32)
        make_identity(nc, ident_f32[:])

        mask = {}
        for smaller in (True, False):
            table = keep.tile([P, P], BF16, name="mask%d" % smaller)
            nc.vector.memset(table[:], NEG)
            for line in range(LINES):
                lo, hi = (0, line * SIDE) if smaller else ((line + 1) * SIDE, P)
                if lo < hi:
                    nc.vector.memset(table[line * SIDE : (line + 1) * SIDE, lo:hi], 0.0)
            mask[smaller] = table

        e_home = {}
        blind_codes = {}
        blind_scales = {}
        for direction in (UP, DOWN):
            smaller = sees_smaller(direction)
            for i in range(TILES):
                e = keep.tile([P, POSITIONS], BF16, name="e%d_%d" % (smaller, i))
                first, behind = seen_keys(direction, i)
                passes = pass_list(direction, i)
                if smaller:
                    lo, hi = behind, (passes[-1] + 1) * K_PASS
                else:
                    lo, hi = passes[0] * K_PASS, first
                nc.gpsimd.memset(e[:, lo:hi], 0.0)
                if i == blind_tile(direction):
                    nc.gpsimd.memset(e[blind_rows(direction), lo:hi], 1.0)
                e_home[(smaller, i)] = e
            ones = keep.tile([P, P, PACK], BF16, name="ones%d" % smaller, align_bytes=64)
            nc.vector.memset(ones[:], 0.0)
            nc.vector.memset(ones[:, blind_rows(direction), :], 1.0)
            codes = keep.tile([P, P], U32, name="blind_codes%d" % smaller, align_bytes=64)
            scales = keep.tile([P, P], U8, name="blind_scales%d" % smaller, align_bytes=64)
            nc.vector.quantize_mx(
                out=codes[:].bitcast(FP8X4),
                scales=scales[:],
                in_=ones[:].rearrange("p w t -> p (w t)"),
            )
            blind_codes[smaller] = codes
            blind_scales[smaller] = scales

        total = keep.tile([P, TILES, CHANNELS], F32)
        out_rows = out[0].rearrange("(i p) c -> p i c", p=P)
        out_columns = out[0].rearrange("(r i l) c -> l r i c", r=SIDE, i=TILES, l=LINES)

        v_grouped = {}
        v_codes = {}
        v_scales = {}
        turned = {}
        q_t = {}
        k_t = {}
        bank_of = {}
        staged_of = {}
        neg_max_of = {}
        row_sum = {}
        divisor = {}
        e_t_of = {}
        pv_of = {}
        e_codes = {}
        e_scales = {}
        grouped_of = {}
        inverse = {}
        side_sum = {}

        def turn_inputs(g, what, tiles=ALL_TILES):
            direction, h = groups[g]
            if what == "q" and not sees_smaller(direction):
                return
            raw = k_raw[direction] if what == "k" else q_raw[in_columns(direction)]
            bank = psum_turn.tile([P, (tiles.stop - tiles.start) * P], BF16, tag="turn")
            for n in range(tiles.stop - tiles.start):
                nc.tensor.transpose(
                    bank[:, n * P : (n + 1) * P],
                    raw[:, tiles.start + n, h * WIDTH : (h + 1) * WIDTH],
                    ident_bf16[:],
                )
            turned[(what, tiles.start)] = bank

        def keep_inputs(g, what, tiles=ALL_TILES):
            direction, h = groups[g]
            if what == "q" and not sees_smaller(direction):
                return
            if tiles.start == 0 and what == "k":
                k_t[g] = operands.tile([P, POSITIONS], BF16, name="k_t", tag="k_t")
            if tiles.start == 0 and what == "q":
                q_t[h] = operands.tile([P, POSITIONS], BF16, name="q_t", tag="q_t")
            kept = k_t[g] if what == "k" else q_t[h]
            part = kept[:, tiles.start * P : tiles.stop * P]
            if g == 0 and what == "q":
                nc.vector.tensor_copy(out=part, in_=turned[(what, tiles.start)][:])
            else:
                nc.scalar.copy(out=part, in_=turned[(what, tiles.start)][:])

        def regroup_values(columns, b, h):
            by_half = (
                v_keys_columns[:].rearrange("p b u x -> p u b x") if columns else v_keys_rows[:]
            )
            head = slice(h * WIDTH, (h + 1) * WIDTH)
            if h == 0:
                v_grouped[b] = work.tile(
                    [P, CHANNELS, HALVES, PAIR], BF16, name="v_grouped", tag="v_grouped", bufs=2, align_bytes=64
                )
            nc.gpsimd.tensor_scalar(
                out=v_grouped[b][:, head],
                in0=by_half[:, b * HALVES : (b + 1) * HALVES, :, head].rearrange("p u b x -> p x u b"),
                scalar1=1.0,
                scalar2=0.0,
                op0=ALU.mult,
                op1=ALU.add,
            )

        def quantise_values(columns):
            codes = keep.tile([P, PASSES * CHANNELS], U32, name="v_codes%d" % columns, align_bytes=64)
            scales = keep.tile([P, PASSES * CHANNELS], U8, name="v_scales%d" % columns, align_bytes=64)
            for b in range(PASSES):
                cols = slice(b * CHANNELS, (b + 1) * CHANNELS)
                nc.vector.quantize_mx(
                    out=codes[:, cols].bitcast(FP8X4),
                    scales=scales[:, cols],
                    in_=v_grouped[b][:].rearrange("p x u b -> p (x u b)"),
                )
            v_codes[columns] = codes
            v_scales[columns] = scales

        def scores(g, i, n):
            direction, h = groups[g]
            smaller = sees_smaller(direction)
            first, behind = seen_keys(direction, i)
            own_lo, own_hi = max(first, i * P), min(behind, (i + 1) * P)
            b = pass_list(direction, i)[n]
            lo = max(first, b * K_PASS)
            hi = min(behind, (b + 1) * K_PASS)
            s_bank = psum_scores.tile([P, K_PASS], F32, tag="scores")
            on_diagonal = lo <= own_lo < hi
            nc.tensor.matmul(
                s_bank[:],
                lhsT=q_t[h][:, i * P : (i + 1) * P],
                rhs=k_t[g][:, b * K_PASS : (b + 1) * K_PASS],
                start=True,
                stop=not on_diagonal,
            )
            if on_diagonal:
                nc.tensor.matmul(
                    s_bank[:, own_lo - b * K_PASS : own_hi - b * K_PASS],
                    lhsT=ident_bf16[:],
                    rhs=mask[smaller][:, own_lo - i * P : own_hi - i * P],
                    start=False,
                    stop=True,
                )
            bank_of[(g, i, n)] = (s_bank[:, lo - b * K_PASS : hi - b * K_PASS], lo, hi)

        def stage_scores(g, i, n):
            in_psum, lo, hi = bank_of[(g, i, n)]
            if n == 0:
                staged_of[(g, i)] = work.tile([P, POSITIONS], F32, name="staged", tag="staged", bufs=6)
            lowest = work.tile([P, 1], F32, bufs=8)
            nc.vector.tensor_scalar(
                out=staged_of[(g, i)][:, lo:hi],
                in0=in_psum,
                scalar1=-1.0,
                scalar2=None if n == 0 else neg_max_of[(g, i)][:, 0:1],
                op0=ALU.mult,
                op1=ALU.min,
                accum_out=lowest[:],
            )
            neg_max_of[(g, i)] = lowest

        def exponential(g, i):
            direction, h = groups[g]
            first, behind = seen_keys(direction, i)
            e = e_home[(sees_smaller(direction), i)]
            if g not in row_sum:
                row_sum[g] = work.tile([P, TILES], F32, name="row_sum", tag="row_sum")
            nc.scalar.activation(
                out=e[:, first:behind],
                in_=staged_of[(g, i)][:, first:behind],
                func=ACT.Exp,
                bias=neg_max_of[(g, i)][:, 0:1],
                scale=-1.0,
                accum_out=row_sum[g][:, i : i + 1],
            )
            if i == blind_tile(direction):
                own_lo, own_hi = max(first, i * P), min(behind, (i + 1) * P)
                nc.gpsimd.memset(e[blind_rows(direction), own_lo:own_hi], 1.0)

        def bank_list(g, quad):
            direction, h = groups[g]
            tiles = orders[g][quad * ROUND : (quad + 1) * ROUND]
            wide = [[(i, 0), (i, 1)] for i in tiles if len(pass_list(direction, i)) == PASSES]
            shared = [(i, 0) for i in tiles if len(pass_list(direction, i)) == 1]
            if g == len(groups) - 1:
                return wide + [shared]
            return [wide[0], shared, wide[1]]

        def quantise_list(g):
            return [[0, 1], [2]] if g == len(groups) - 1 else [[0], [1, 2]]

        def turn(g, i, n):
            direction, h = groups[g]
            quad = orders[g].index(i) // ROUND
            e_words = e_home[(sees_smaller(direction), i)][:].bitcast(F32)
            b = pass_list(direction, i)[n]
            for bank, passes in enumerate(bank_list(g, quad)):
                if (i, n) in passes:
                    if (g, quad, bank) not in e_t_of:
                        e_t_of[(g, quad, bank)] = psum_turn.tile(
                            [P, PASSES, HALVES, P], F32, name="e_t", tag="turn"
                        )
                    for u in range(HALVES):
                        w0 = (b * HALVES + u) * P
                        nc.tensor.transpose(
                            e_t_of[(g, quad, bank)][:, passes.index((i, n)), u, :],
                            e_words[:, w0 : w0 + P],
                            ident_f32[:],
                        )

        def regroup(g, quad, bank):
            for banks in quantise_list(g):
                if bank not in banks:
                    continue
                key = (g, quad, banks[0])
                if key not in grouped_of:
                    grouped_of[key] = work.tile(
                        [P, len(banks), PASSES * K_PASS],
                        BF16,
                        name="grouped",
                        tag="grouped%d" % len(banks),
                        align_bytes=64,
                    )
                nc.scalar.copy(
                    out=grouped_of[key][:, banks.index(bank)]
                    .bitcast(F32)
                    .rearrange("p (n w u) -> p n w u", n=PASSES, u=HALVES),
                    in_=e_t_of[(g, quad, bank)][:].rearrange("p n u w -> p n w u"),
                )

        def quantise(g, quad, banks):
            if g not in e_codes:
                e_codes[g] = operands.tile(
                    [P, GROUP_SLOTS * P], U32, name="e_codes", tag="e_codes", align_bytes=64
                )
                e_scales[g] = operands.tile(
                    [P, GROUP_SLOTS * P], U8, name="e_scales", tag="e_scales", align_bytes=64
                )
            lo = quad * GROUP_SLOTS // 2 + banks[0] * PASSES
            words = slice(lo * P, (lo + len(banks) * PASSES) * P)
            nc.vector.quantize_mx(
                out=e_codes[g][:, words].bitcast(FP8X4),
                scales=e_scales[g][:, words],
                in_=grouped_of[(g, quad, banks[0])][:].rearrange("p n k -> p (n k)"),
            )

        def place(g, i, n):
            quad = orders[g].index(i) // ROUND
            in_order = [which for passes in bank_list(g, quad) for which in passes]
            return quad * GROUP_SLOTS // 2 + in_order.index((i, n))

        def prepare_sums(g):
            direction, h = groups[g]
            blind = blind_tile(direction)
            nc.gpsimd.memset(row_sum[g][blind_rows(direction), blind : blind + 1], float(POSITIONS))
            divisor[g] = row_sum[g]
            if in_columns(direction):
                divisor[g] = work.tile([P, TILES], F32, name="divisor", tag="divisor")
                nc.gpsimd.tensor_scalar(
                    out=divisor[g][:], in0=row_sum[g][:], scalar1=5.0, scalar2=0.0, op0=ALU.mult, op1=ALU.add
                )

        def normalise(g):
            inverse[g] = work.tile([P, TILES], F32, name="inverse", tag="inverse")
            nc.vector.reciprocal(out=inverse[g][:], in_=divisor[g][:])

        def weighted_values(g, tiles, last):
            direction, h = groups[g]
            smaller = sees_smaller(direction)
            columns = in_columns(direction)
            if last:
                pv = psum_scores.tile([P, ROUND, WIDTH], F32, name="pv_last", tag="scores")
            else:
                pv = psum_pv.tile([P, ROUND, WIDTH], F32, name="pv", tag="pv")
            for n, i in enumerate(tiles):
                passes = pass_list(direction, i)
                lhs = []
                for m, b in enumerate(passes):
                    at = place(g, i, m)
                    words = slice(at * P, (at + 1) * P)
                    lhs.append((b, e_codes[g][:, words], e_scales[g][:, words]))
                if i == blind_tile(direction):
                    lhs.append((PASSES - 1 - passes[0], blind_codes[smaller][:], blind_scales[smaller][:]))
                for k, (b, codes, scales) in enumerate(lhs):
                    of_v = slice(b * CHANNELS + h * WIDTH, b * CHANNELS + (h + 1) * WIDTH)
                    nc.tensor.matmul_mx(
                        out=pv[:, n, :],
                        lhsT=codes.bitcast(FP8X4),
                        lhsT_scale=scales,
                        rhs=v_codes[columns][:, of_v].bitcast(FP8X4),
                        rhs_scale=v_scales[columns][:, of_v],
                        start=(k == 0),
                        stop=(k == len(lhs) - 1),
                    )
            pv_of[(g, tiles[0])] = pv

        def sum_up(g, tiles):
            direction, h = groups[g]
            head = slice(h * WIDTH, (h + 1) * WIDTH)
            pv = pv_of[(g, tiles[0])]
            if direction == UP and tiles[0] == orders[g][0]:
                side_sum[h] = work.tile([P, TILES, WIDTH], F32, name="side_sum", tag="side_sum", bufs=2)
            for n, i in enumerate(tiles):
                acc = total[:, i, head] if in_columns(direction) else side_sum[h][:, i, :]
                so_far = v_rows[:, i, head] if direction == UP else acc
                nc.vector.scalar_tensor_tensor(
                    out=acc,
                    in0=pv[:, n, :],
                    scalar=inverse[g][:, i : i + 1],
                    in1=so_far,
                    op0=ALU.mult,
                    op1=ALU.add,
                )
            if direction == RIGHT:
                for first, behind in runs(tiles):
                    for line in range(LINES):
                        nc.sync.dma_start(
                            out=out_columns[line][:, first:behind, head],
                            in_=total[line * SIDE : (line + 1) * SIDE, first:behind, head],
                        )

        def park(h):
            head = slice(h * WIDTH, (h + 1) * WIDTH)
            nc.sync.dma_start(out=out_rows[:, :, head], in_=side_sum[h][:])

        def fetch(h):
            head = slice(h * WIDTH, (h + 1) * WIDTH)
            for line in range(LINES):
                nc.sync.dma_start(
                    out=total[line * SIDE : (line + 1) * SIDE, :, head], in_=out_columns[line][:, :, head]
                )

        def take_fifth(h, first):
            part = total[:, first : first + FIFTH_TILES, h * WIDTH : (h + 1) * WIDTH]
            nc.gpsimd.tensor_scalar(out=part, in0=part, scalar1=0.2, scalar2=0.0, op0=ALU.mult, op1=ALU.add)

        slots = []
        exponentials, regroups, quantises = {}, {}, {}
        for g, (direction, h) in enumerate(groups):
            for pair in range(TILES // 2):
                tiles = sorted(orders[g][2 * pair : 2 * pair + 2], key=lambda i: -len(pass_list(direction, i)))
                for n in range(PASSES):
                    slots += [(g, i, n) for i in tiles if n < len(pass_list(direction, i))]
            for i in orders[g]:
                last = slots.index((g, i, len(pass_list(direction, i)) - 1))
                exponentials.setdefault(last + EXP_LAG, []).append((g, i))
            for quad in range(TILES // ROUND):
                ready = []
                for passes in bank_list(g, quad):
                    ready.append(max(slots.index((g, i, n)) for i, n in passes))
                    regroups.setdefault(ready[-1] + TURN_LAG, []).append((g, quad, len(ready) - 1))
                for banks in quantise_list(g):
                    last = max(ready[n] for n in banks)
                    quantises.setdefault(last + QUANT_LAG, []).append((g, quad, banks))

        for half in HALF_TILES:
            for what in ("q", "k"):
                turn_inputs(0, what, half)
            for what in ("q", "k"):
                keep_inputs(0, what, half)
        for ahead in range(SCORE_LEAD):
            scores(*slots[ahead])
        for slot in range(len(slots) + DRAIN):
            g, position = divmod(slot, GROUP_SLOTS)
            if slot + SCORE_LEAD < len(slots):
                scores(*slots[slot + SCORE_LEAD])
            if slot < len(slots):
                stage_scores(*slots[slot])
            if 0 <= slot - TURN_LAG < len(slots):
                turn(*slots[slot - TURN_LAG])
            for which in exponentials.get(slot, []):
                exponential(*which)
            for which in regroups.get(slot, []):
                regroup(*which)
            for which in quantises.get(slot, []):
                quantise(*which)

            if g + 1 < len(groups):
                if position == AT_TURN_KEYS:
                    turn_inputs(g + 1, "k")
                if position == AT_KEEP_KEYS:
                    keep_inputs(g + 1, "k")
                if position == AT_TURN_QUERIES:
                    turn_inputs(g + 1, "q")
                if position == AT_KEEP_QUERIES:
                    keep_inputs(g + 1, "q")
            if g == 0 and position < PASSES * HEADS:
                regroup_values(False, position // HEADS, position % HEADS)
            pass_of_v = g - (len(groups) // 2 - PASSES)
            if 0 <= pass_of_v < PASSES and position % (GROUP_SLOTS // HEADS) == 0:
                regroup_values(True, pass_of_v, position // (GROUP_SLOTS // HEADS))
            if g in (1, len(groups) // 2) and position == AT_QUANTISE_VALUES:
                quantise_values(g > 1)
            for ended in range(max(0, g - 4), min(g, len(groups))):
                since = slot - (ended + 1) * GROUP_SLOTS
                direction, h = groups[ended]
                rounds = rounds_of(ended)
                if since == AT_PREPARE_SUMS:
                    prepare_sums(ended)
                if since == AT_NORMALISE:
                    normalise(ended)
                for tiles, at_products, at_sums in rounds:
                    last = ended == len(groups) - 1 and tiles[-1] == orders[ended][-1]
                    if since == at_products:
                        weighted_values(ended, tiles, last)
                    if since == at_sums:
                        sum_up(ended, tiles)
                if direction == DOWN and since == AT_PARK:
                    park(h)
                if direction == DOWN and since == AT_FETCH:
                    fetch(h)
                if direction == DOWN and AT_FIFTH <= since < AT_FIFTH + TILES // FIFTH_TILES:
                    take_fifth(h, (since - AT_FIFTH) * FIFTH_TILES)
